import numpy as np
import ml_dtypes


def mxq(x, axis, fmt="e4m3"):
    dtype, down = {"e4m3": (ml_dtypes.float8_e4m3fn, 7), "e5m2": (ml_dtypes.float8_e5m2, 14)}[fmt]
    v = np.moveaxis(np.asarray(x, np.float32).astype(ml_dtypes.bfloat16).astype(np.float64), axis, -1)
    blocks = v.reshape(v.shape[:-1] + (-1, 32))
    amax = np.abs(blocks).max(-1, keepdims=True)
    byte = np.maximum(np.where(amax > 0, np.frexp(amax)[1] - 1 + 127, 0) - down, 1)
    scale = np.exp2(byte - 127.0)
    codes = (blocks / scale).astype(np.float32).astype(dtype).astype(np.float64)
    return np.moveaxis((codes * scale).reshape(v.shape), -1, axis)


WIDE = False


def mx_kscale(k):
    if not WIDE:
        return np.ones(k)
    levels = np.array([10, -10, 5, -5, 0])
    if k % 512:
        return np.exp2(np.random.permutation(np.resize(levels, k // 32))).repeat(32)
    a = np.empty((k // 512, 16))
    for p in range(k // 512):
        a[p, :8] = np.random.permutation(np.resize(levels, 8))
        for g in range(8):
            far = levels[np.abs(levels - a[p, g]) >= 10]
            a[p, g + 8] = far[np.random.randint(len(far))]
    return np.exp2(a.ravel()).repeat(32)


BF16 = ml_dtypes.bfloat16


def bf(x):
    return np.asarray(x, np.float32).astype(BF16)


def f64(x):
    return np.asarray(x).astype(np.float64)


B, S, D, HD = 4, 2048, 512, 128
HALF = HD // 2


def rotate_half(t):
    return np.concatenate((-t[..., HALF:], t[..., :HALF]), axis=-1)


def rope_cos_sin():
    inv_freq = 1.0 / (10000.0 ** (np.arange(0, HD, 2, dtype=np.float64) / HD))
    freqs = np.arange(S, dtype=np.float64)[:, None] * inv_freq[None, :]
    emb = np.concatenate((freqs, freqs), axis=-1)
    return np.cos(emb), np.sin(emb)


def draw0():
    s = mx_kscale(D)
    return {"x": bf(np.random.standard_normal((B, S, D)) * s),
            "w_q": bf(np.random.standard_normal((HD, D)) / np.sqrt(D) / s[None, :]),
            "w_k": bf(np.random.standard_normal((HD, D)) / np.sqrt(D) / s[None, :]),
            "w_v": bf(np.random.standard_normal((HD, D)) / np.sqrt(D) / s[None, :])}


def core(x, w_q, w_k, w_v):
    xq = mxq(f64(x), 2, "e4m3")
    q = xq @ mxq(f64(w_q), 1, "e4m3").T
    k = xq @ mxq(f64(w_k), 1, "e4m3").T
    v = xq @ mxq(f64(w_v), 1, "e4m3").T
    cos, sin = rope_cos_sin()
    q_rot = q * cos + rotate_half(q) * sin
    k_rot = k * cos + rotate_half(k) * sin
    return q_rot, k_rot, v


def e4m3fn_bytes(y):
    return np.clip(np.asarray(y, np.float64), -448.0, 448.0).astype(np.float32).astype(ml_dtypes.float8_e4m3fn).view(np.uint8)


def e4m3fn_values(b):
    return np.asarray(b, np.uint8).view(ml_dtypes.float8_e4m3fn).astype(np.float64)


def setup_inputs():
    d = draw0()
    x0 = np.asarray(d['x']).astype(np.float64)
    s = (np.max(np.abs(x0), axis=(0, 1), keepdims=True) / 448.0).astype(np.float32)
    out = {}
    for k, v in d.items():
        if k == 'x':
            out['x_bytes'] = e4m3fn_bytes(x0 / s.astype(np.float64))
            out['x_scale'] = s
        else:
            out[k] = v
    return out


def reference(x_bytes, x_scale, w_q, w_k, w_v):
    return core(e4m3fn_values(x_bytes) * x_scale.astype(np.float64), w_q, w_k, w_v)

@@ -1,0 +1,277 @@
+from contextlib import ExitStack
+
+import concourse.mybir as mybir
+from concourse.masks import make_identity
+
+B, S, D, HD = 4, 2048, 512, 128
+HALF = HD // 2
+FLOPS = 2 * B * S * D * 3 * HD
+
+F32 = mybir.dt.float32
+BF16 = mybir.dt.bfloat16
+I32 = mybir.dt.int32
+U32 = mybir.dt.uint32
+U8 = mybir.dt.uint8
+FP8 = mybir.dt.float8_e4m3fn
+FP8X4 = mybir.dt.float8_e4m3fn_x4
+ALU = mybir.AluOpType
+ACT = mybir.ActivationFunctionType
+
+P = 128
+NI = S // P
+GT = 4
+NG = B * NI // GT
+PI = 3.141592653589793
+RATIO = 10000.0 ** (-1.0 / HALF)
+MAGIC = 8388608.0
+YSET = frozenset(n for n in range(1, NG) if n % 2 == 1)
+
+
+def tile_ropemaskedattentionhead_pa_t_kernel(tc, x_bytes, x_scale, w_q, w_k, w_v, out_0, out_1, out_2):
+    nc = tc.nc
+    with ExitStack() as ctx:
+        const = ctx.enter_context(tc.tile_pool(name="const", bufs=1))
+        work = ctx.enter_context(tc.tile_pool(name="work", bufs=3))
+        ps_t = ctx.enter_context(tc.psum_pool(name="ps_t", bufs=2))
+        ps_y = ctx.enter_context(tc.psum_pool(name="ps_y", bufs=1))
+        ps_r = ctx.enter_context(tc.psum_pool(name="ps_r", bufs=4))
+        ps_v = ctx.enter_context(tc.psum_pool(name="ps_v", bufs=1))
+
+        x_views = [x_bytes[b].rearrange("(p i) k -> p (i k)", i=NI) for b in range(B)]
+        o_views = [[o[b].rearrange("(p i) d -> p (i d)", i=NI) for b in range(B)] for o in (out_0, out_1, out_2)]
+
+        xb = const.tile([P, NG * GT * D], U8, name="xb")
+        XW = GT * D
+
+        def load(n, pieces):
+            b, g = divmod(n, NI // GT)
+            step = XW // pieces
+            for c in range(pieces):
+                nc.sync.dma_start(out=xb[:, n * XW + c * step:n * XW + (c + 1) * step],
+                                  in_=x_views[b][:, g * XW + c * step:g * XW + (c + 1) * step])
+
+        load(0, 2)
+        w_a = const.tile([P, D], BF16, name="w_a")
+        w_b = const.tile([P, D], BF16, name="w_b")
+        w_c = const.tile([P, D], BF16, name="w_c")
+        sc4 = const.tile([P, 4], F32, name="sc4")
+        nc.sync.dma_start(out=w_a[0:HALF, :], in_=w_q[HALF:HD, :])
+        nc.sync.dma_start(out=w_a[HALF:P, :], in_=w_k[HALF:HD, :])
+        nc.sync.dma_start(out=w_b[0:HALF, :], in_=w_q[0:HALF, :])
+        nc.sync.dma_start(out=w_b[HALF:P, :], in_=w_k[0:HALF, :])
+        nc.sync.dma_start(out=w_c[:], in_=w_v[:, :])
+        with nc.allow_non_contiguous_dma(reason="four scales to a partition"):
+            nc.sync.dma_start(out=sc4[:], in_=x_scale.rearrange("a b (p t) -> p (a b t)", t=4))
+        for n in range(1, NG):
+            load(n, 1)
+
+        idx_i = const.tile([P, NI], I32, name="idx_i")
+        nc.gpsimd.iota(idx_i[:], pattern=[[1, NI]], base=0, channel_multiplier=NI)
+        ident = const.tile([P, P], F32, name="ident")
+        make_identity(nc, ident[:])
+        ident_b = const.tile([P, P], BF16, name="ident_b")
+        make_identity(nc, ident_b[:])
+        one = const.tile([P, 1], F32, name="one")
+        nc.vector.memset(one[:], 1.0)
+        junk = const.tile([P, 1], F32, name="junk")
+        nc.scalar.activation(out=junk[:], in_=one[:], func=ACT.Sin)
+
+        st = {}
+
+        def cast(n, pieces):
+            xbf = work.tile([P, XW], BF16, name="xbf", tag="xbf")
+            step = XW // pieces
+            for c in range(pieces):
+                nc.scalar.copy(out=xbf[:, c * step:(c + 1) * step],
+                               in_=xb[:, n * XW + c * step:n * XW + (c + 1) * step].bitcast(FP8))
+            st[("xbf", n)] = xbf
+
+        def turn(n):
+            words = st[("xbf", n)][:].bitcast(F32)
+            for h in range(1 if n in YSET else 2):
+                tp = ps_t.tile([P, 512], F32, name="tp", tag="tp")
+                for a2 in range(2):
+                    a = 2 * h + a2
+                    for u in range(2):
+                        nc.tensor.transpose(tp[:, u * 256 + a2 * P:u * 256 + (a2 + 1) * P],
+                                            words[:, 256 * a + u:256 * (a + 1):2], ident[:])
+                st[("tp", n, h)] = tp
+
+        def turn_y(n):
+            xbf = st[("xbf", n)]
+            tpb = ps_y.tile([P, 1024], BF16, name="tpb", tag="tpb")
+            for a2 in range(2):
+                a = 2 + a2
+                for t in range(4):
+                    nc.tensor.transpose(tpb[:, t * 256 + a2 * P:t * 256 + (a2 + 1) * P],
+                                        xbf[:, a * D + t:(a + 1) * D:4], ident_b[:])
+            pl = work.tile([P, 4, 256], BF16, name="pl", tag="pl")
+            for t in range(4):
+                nc.scalar.activation(out=pl[:, t, :], in_=tpb[:, t * 256:(t + 1) * 256], func=ACT.Copy, scale=sc4[:, t:t + 1])
+            st[("pl", n)] = pl
+
+        def weave(n):
+            nc.scalar.copy(out=st[("grp", n)][:, 1024:2048].rearrange("p (c i t) -> p c t i", i=4, t=4),
+                           in_=st[("pl", n)][:].rearrange("p t (c i) -> p c t i", i=4))
+
+        def x_side(n):
+            scale_out(n, 0)
+            if n in YSET:
+                weave(n)
+            else:
+                scale_out(n, 1)
+
+        def turns_of(n):
+            turn(n)
+            if n in YSET:
+                turn_y(n)
+
+        def scale_out(n, h):
+            if h == 0:
+                st[("grp", n)] = work.tile([P, GT * P * 4], BF16, name="grp", tag="grp", align_bytes=64)
+            grp = st[("grp", n)]
+            nc.vector.tensor_tensor(
+                out=grp[:, h * 1024:(h + 1) * 1024].rearrange("p (r u e) -> p r u e", u=2, e=2),
+                in0=st[("tp", n, h)][:].bitcast(BF16).rearrange("p (u r e) -> p r u e", u=2, e=2),
+                in1=sc4[:].rearrange("p (u e) -> p u e", u=2).unsqueeze(1).to_broadcast([P, 256, 2, 2]),
+                op=ALU.mult)
+
+        def quant(n):
+            codes = work.tile([P, GT * P], U32, name="codes", tag="codes", align_bytes=64)
+            xs = work.tile([P, GT * P], U8, name="xs", tag="xs", align_bytes=64)
+            nc.vector.quantize_mx(out=codes[:].bitcast(FP8X4), scales=xs[:], in_=st[("grp", n)][:])
+            st[("codes", n)] = codes
+            st[("xs", n)] = xs
+
+        def mult(n):
+            codes, xs = st[("codes", n)], st[("xs", n)]
+            vb = ps_v.tile([P, GT * HD], F32, name="vb", tag="vb")
+            st[("vb", n)] = vb
+            for a in range(GT):
+                mm = ps_r.tile([P, 384], F32, name="mm", tag="mm")
+                st[("mm", n, a)] = mm
+                lt = codes[:, a * P:(a + 1) * P].bitcast(FP8X4)
+                ls = xs[:, a * P:(a + 1) * P]
+                nc.tensor.matmul_mx(out=mm[:, 0:256], lhsT=lt, lhsT_scale=ls, rhs=wc[:, 0:256].bitcast(FP8X4),
+                                    rhs_scale=ws[:, 0:256], start=True, stop=True)
+                nc.tensor.matmul_mx(out=mm[:, 256:384], lhsT=lt, lhsT_scale=ls, rhs=wc[:, 0:128].bitcast(FP8X4),
+                                    rhs_scale=ws[:, 0:128], start=True, stop=False)
+                nc.tensor.matmul_mx(out=mm[:, 256:384], lhsT=lt, lhsT_scale=ls, rhs=wc[:, 128:256].bitcast(FP8X4),
+                                    rhs_scale=ws[:, 128:256], start=False, stop=True)
+                nc.tensor.matmul_mx(out=vb[:, a * HD:(a + 1) * HD], lhsT=lt, lhsT_scale=ls,
+                                    rhs=wc[:, 256:384].bitcast(FP8X4), rhs_scale=ws[:, 256:384], start=True, stop=True)
+
+        def rope(n, a):
+            if a == 0:
+                st[("prod", n)] = work.tile([P, GT, 2, 3, HALF], F32, name="prod", tag="prod")
+            prod = st[("prod", n)]
+            i = (n % (NI // GT)) * GT + a
+            nc.vector.tensor_tensor(
+                out=prod[:, a, :, :, :].rearrange("p w c j -> p c w j"),
+                in0=st[("mm", n, a)][:].rearrange("p (c w j) -> p c w j", c=3, w=2),
+                in1=tab[:, i, :, :].unsqueeze(2).to_broadcast([P, 3, 2, HALF]),
+                op=ALU.mult)
+
+        def add_up(n, a0, a1, w0, w1, eng):
+            if a0 == 0 and w0 == 0:
+                st[("o_r", n)] = work.tile([P, 2, GT * HD], F32, name="o_r", tag="o_r")
+            b, g = divmod(n, NI // GT)
+            o_r, prod = st[("o_r", n)], st[("prod", n)]
+            eng.tensor_tensor(
+                out=o_r[:, w0:w1, a0 * HD:a1 * HD].rearrange("p w (a h j) -> p a w h j", h=2, j=HALF),
+                in0=prod[:, a0:a1, w0:w1, 0:2, :],
+                in1=prod[:, a0:a1, w0:w1, 2:3, :].to_broadcast([P, a1 - a0, w1 - w0, 2, HALF]), op=ALU.add)
+            for w in range(w0, w1):
+                nc.sync.dma_start(out=o_views[w][b][:, (g * GT + a0) * HD:(g * GT + a1) * HD], in_=o_r[:, w, a0 * HD:a1 * HD])
+
+        def finish_v(n):
+            b, g = divmod(n, NI // GT)
+            o_v = work.tile([P, GT * HD], F32, name="o_v", tag="o_v")
+            nc.scalar.copy(out=o_v[:], in_=st[("vb", n)][:])
+            nc.sync.dma_start(out=o_views[2][b][:, g * GT * HD:(g + 1) * GT * HD], in_=o_v[:])
+
+        def table(c):
+            rows = slice(c * GT, (c + 1) * GT)
+            nc.scalar.activation(out=sin_t[:, rows, :], in_=frac[:, rows, :], func=ACT.Sin, scale=2.0 * PI)
+            nc.scalar.activation(out=nsin_t[:, rows, :], in_=frac[:, rows, :], func=ACT.Sin, scale=-2.0 * PI)
+            nc.scalar.activation(out=absf[:, rows, :], in_=frac[:, rows, :], func=ACT.Abs)
+            nc.scalar.activation(out=tab[:, rows, 2, :], in_=absf[:, rows, :], func=ACT.Sin, scale=-2.0 * PI, bias=0.5 * PI)
+            nc.gpsimd.tensor_tensor(out=tab[:, rows, 1, :], in0=sin_t[:, rows, :], in1=tab[:, rows, 2, :], op=ALU.subtract)
+            nc.gpsimd.tensor_tensor(out=tab[:, rows, 0, :], in0=nsin_t[:, rows, :], in1=tab[:, rows, 2, :], op=ALU.subtract)
+
+        pos = const.tile([P, NI], F32, name="pos")
+        nc.vector.tensor_copy(out=pos[:], in_=idx_i[:])
+        turns = const.tile([P, HALF], F32, name="turns")
+        nc.vector.tensor_scalar(out=turns[:, 0:1], in0=one[:], scalar1=0.5 / PI, scalar2=None, op0=ALU.mult)
+        for m in range(6):
+            w = 1 << m
+            nc.vector.tensor_scalar(out=turns[:, w:2 * w], in0=turns[:, 0:w], scalar1=RATIO ** w, scalar2=None, op0=ALU.mult)
+        ang = const.tile([P, NI, HALF], F32, name="ang")
+        nc.vector.tensor_tensor(out=ang[:], in0=pos[:].unsqueeze(2).to_broadcast([P, NI, HALF]),
+                                in1=turns[:].unsqueeze(1).to_broadcast([P, NI, HALF]), op=ALU.mult)
+        whole = const.tile([P, NI, HALF], I32, name="whole")
+        nc.vector.tensor_scalar(out=whole[:], in0=ang[:], scalar1=MAGIC, scalar2=MAGIC, op0=ALU.add, op1=ALU.subtract)
+        frac = const.tile([P, NI, HALF], F32, name="frac")
+        nc.vector.tensor_tensor(out=frac[:], in0=ang[:], in1=whole[:], op=ALU.subtract)
+        sin_t = const.tile([P, NI, HALF], F32, name="sin_t")
+        nsin_t = const.tile([P, NI, HALF], F32, name="nsin_t")
+        absf = const.tile([P, NI, HALF], F32, name="absf")
+        tab = const.tile([P, NI, 3, HALF], F32, name="tab")
+
+        wc = const.tile([P, 384], U32, name="wc", align_bytes=64)
+        ws = const.tile([P, 384], U8, name="ws", align_bytes=64)
+        wg_ab = const.tile([P, 1024], BF16, name="wg_ab", align_bytes=64)
+        wg_c = const.tile([P, 512], BF16, name="wg_c", align_bytes=64)
+        tw = ps_r.tile([P, 512], F32, name="tw", tag="mm")
+        for a2, w_t in enumerate((w_a, w_b)):
+            for u in range(2):
+                nc.tensor.transpose(tw[:, u * 256 + a2 * P:u * 256 + (a2 + 1) * P], w_t[:].bitcast(F32)[:, u:256:2], ident[:])
+        tw2 = ps_r.tile([P, 512], F32, name="tw2", tag="mm")
+        for u in range(2):
+            nc.tensor.transpose(tw2[:, u * P:(u + 1) * P], w_c[:].bitcast(F32)[:, u:256:2], ident[:])
+        cast(0, 4)
+        turns_of(0)
+        nc.vector.tensor_copy(out=wg_ab[:].bitcast(F32).rearrange("p (r u) -> p r u", u=2),
+                              in_=tw[:].rearrange("p (u r) -> p r u", u=2))
+        nc.vector.tensor_copy(out=wg_c[:].bitcast(F32).rearrange("p (r u) -> p r u", u=2),
+                              in_=tw2[:, 0:256].rearrange("p (u r) -> p r u", u=2))
+        table(0)
+        scale_out(0, 0)
+        cast(1, 2)
+        nc.vector.quantize_mx(out=wc[:, 0:256].bitcast(FP8X4), scales=ws[:, 0:256], in_=wg_ab[:])
+        scale_out(0, 1)
+        nc.vector.quantize_mx(out=wc[:, 256:384].bitcast(FP8X4), scales=ws[:, 256:384], in_=wg_c[:])
+        turns_of(1)
+        quant(0)
+        mult(0)
+        table(1)
+        cast(2, 1)
+        x_side(1)
+        turns_of(2)
+        cast(3, 1)
+
+        with tc.manual_schedule(engines={mybir.EngineType.DVE}):
+            for n in range(NG):
+                last = n + 1 == NG
+                finish_v(n)
+                rope(n, 0)
+                rope(n, 1)
+                if last:
+                    add_up(n, 0, 2, 0, 2, nc.gpsimd)
+                rope(n, 2)
+                rope(n, 3)
+                if last:
+                    add_up(n, 2, 4, 0, 2, nc.vector)
+                else:
+                    add_up(n, 0, 4, 0, 1, nc.gpsimd)
+                    add_up(n, 0, 4, 1, 2, nc.gpsimd)
+                    quant(n + 1)
+                    mult(n + 1)
+                if n + 2 < NG:
+                    x_side(n + 2)
+                if n + 3 < NG:
+                    turns_of(n + 3)
+                if n + 2 < NI // GT:
+                    table(n + 2)
+                if n + 4 < NG:
+                    cast(n + 4, 1)

@@ -190,6 +190,12 @@ def tile_ropemaskedattentionhead_pa_t_kernel(tc, x_bytes, x_scale, w_q, w_k, w_v
             nc.scalar.copy(out=o_v[:], in_=st[("vb", n)][:])
             nc.sync.dma_start(out=o_views[2][b][:, g * GT * HD:(g + 1) * GT * HD], in_=o_v[:])
 
+        def idle(n):
+            dm = ps_v.tile([P, GT * HD], F32, name="dm", tag="vb")
+            for r in range(2):
+                nc.tensor.matmul_mx(out=dm[:], lhsT=wc[:, 0:128].bitcast(FP8X4), lhsT_scale=ws[:, 0:128],
+                                    rhs=st[("codes", n)][:].bitcast(FP8X4), rhs_scale=st[("xs", n)][:], start=True, stop=True)
+
         def table(c):
             rows = slice(c * GT, (c + 1) * GT)
             nc.scalar.activation(out=sin_t[:, rows, :], in_=frac[:, rows, :], func=ACT.Sin, scale=2.0 * PI)
@@ -254,6 +260,8 @@ def tile_ropemaskedattentionhead_pa_t_kernel(tc, x_bytes, x_scale, w_q, w_k, w_v
             for n in range(NG):
                 last = n + 1 == NG
                 finish_v(n)
+                if not last:
+                    idle(n)
                 rope(n, 0)
                 rope(n, 1)
                 if last:

@@ -24,7 +24,8 @@ NG = B * NI // GT
 PI = 3.141592653589793
 RATIO = 10000.0 ** (-1.0 / HALF)
 MAGIC = 8388608.0
-YSET = frozenset(n for n in range(1, NG) if n % 2 == 1)
+VCAST = frozenset((0,))
+YSET = frozenset((3, 5, 7, 9, 11, 12, 13, 14, 15))
 
 
 def tile_ropemaskedattentionhead_pa_t_kernel(tc, x_bytes, x_scale, w_q, w_k, w_v, out_0, out_1, out_2):
@@ -82,8 +83,12 @@ def tile_ropemaskedattentionhead_pa_t_kernel(tc, x_bytes, x_scale, w_q, w_k, w_v
             xbf = work.tile([P, XW], BF16, name="xbf", tag="xbf")
             step = XW // pieces
             for c in range(pieces):
-                nc.scalar.copy(out=xbf[:, c * step:(c + 1) * step],
-                               in_=xb[:, n * XW + c * step:n * XW + (c + 1) * step].bitcast(FP8))
+                if n in VCAST:
+                    nc.vector.tensor_copy(out=xbf[:, c * step:(c + 1) * step],
+                                          in_=xb[:, n * XW + c * step:n * XW + (c + 1) * step].bitcast(FP8))
+                else:
+                    nc.scalar.copy(out=xbf[:, c * step:(c + 1) * step],
+                                   in_=xb[:, n * XW + c * step:n * XW + (c + 1) * step].bitcast(FP8))
             st[("xbf", n)] = xbf
 
         def turn(n):
@@ -199,11 +204,12 @@ def tile_ropemaskedattentionhead_pa_t_kernel(tc, x_bytes, x_scale, w_q, w_k, w_v
         def table(c):
             rows = slice(c * GT, (c + 1) * GT)
             nc.scalar.activation(out=sin_t[:, rows, :], in_=frac[:, rows, :], func=ACT.Sin, scale=2.0 * PI)
-            nc.scalar.activation(out=nsin_t[:, rows, :], in_=frac[:, rows, :], func=ACT.Sin, scale=-2.0 * PI)
-            nc.scalar.activation(out=absf[:, rows, :], in_=frac[:, rows, :], func=ACT.Abs)
-            nc.scalar.activation(out=tab[:, rows, 2, :], in_=absf[:, rows, :], func=ACT.Sin, scale=-2.0 * PI, bias=0.5 * PI)
-            nc.gpsimd.tensor_tensor(out=tab[:, rows, 1, :], in0=sin_t[:, rows, :], in1=tab[:, rows, 2, :], op=ALU.subtract)
-            nc.gpsimd.tensor_tensor(out=tab[:, rows, 0, :], in0=nsin_t[:, rows, :], in1=tab[:, rows, 2, :], op=ALU.subtract)
+            nc.scalar.activation(out=half_t[:, rows, :], in_=frac[:, rows, :], func=ACT.Sin, scale=PI)
+            nc.gpsimd.tensor_tensor(out=sq_t[:, rows, :], in0=half_t[:, rows, :], in1=half_t[:, rows, :], op=ALU.mult)
+            nc.gpsimd.tensor_scalar(out=ncos_t[:, rows, :], in0=sq_t[:, rows, :], scalar1=2.0, scalar2=-1.0, op0=ALU.mult, op1=ALU.add)
+            nc.gpsimd.tensor_scalar(out=tab[:, rows, 2, :], in0=sq_t[:, rows, :], scalar1=-2.0, scalar2=1.0, op0=ALU.mult, op1=ALU.add)
+            nc.gpsimd.tensor_tensor(out=tab[:, rows, 0, :], in0=ncos_t[:, rows, :], in1=sin_t[:, rows, :], op=ALU.subtract)
+            nc.gpsimd.tensor_tensor(out=tab[:, rows, 1, :], in0=ncos_t[:, rows, :], in1=sin_t[:, rows, :], op=ALU.add)
 
         pos = const.tile([P, NI], F32, name="pos")
         nc.vector.tensor_copy(out=pos[:], in_=idx_i[:])
@@ -220,8 +226,9 @@ def tile_ropemaskedattentionhead_pa_t_kernel(tc, x_bytes, x_scale, w_q, w_k, w_v
         frac = const.tile([P, NI, HALF], F32, name="frac")
         nc.vector.tensor_tensor(out=frac[:], in0=ang[:], in1=whole[:], op=ALU.subtract)
         sin_t = const.tile([P, NI, HALF], F32, name="sin_t")
-        nsin_t = const.tile([P, NI, HALF], F32, name="nsin_t")
-        absf = const.tile([P, NI, HALF], F32, name="absf")
+        half_t = const.tile([P, NI, HALF], F32, name="half_t")
+        sq_t = const.tile([P, NI, HALF], F32, name="sq_t")
+        ncos_t = const.tile([P, NI, HALF], F32, name="ncos_t")
         tab = const.tile([P, NI, 3, HALF], F32, name="tab")
 
         wc = const.tile([P, 384], U32, name="wc", align_bytes=64)
@@ -235,7 +242,7 @@ def tile_ropemaskedattentionhead_pa_t_kernel(tc, x_bytes, x_scale, w_q, w_k, w_v
         tw2 = ps_r.tile([P, 512], F32, name="tw2", tag="mm")
         for u in range(2):
             nc.tensor.transpose(tw2[:, u * P:(u + 1) * P], w_c[:].bitcast(F32)[:, u:256:2], ident[:])
-        cast(0, 4)
+        cast(0, 2)
         turns_of(0)
         nc.vector.tensor_copy(out=wg_ab[:].bitcast(F32).rearrange("p (r u) -> p r u", u=2),
                               in_=tw[:].rearrange("p (u r) -> p r u", u=2))

@@ -21,18 +21,21 @@ P = 128
 NI = S // P
 GT = 4
 NG = B * NI // GT
+NM = 2 * NG
 PI = 3.141592653589793
 RATIO = 10000.0 ** (-1.0 / HALF)
 MAGIC = 8388608.0
 VCAST = frozenset((0,))
-YSET = frozenset((3, 5, 7, 9, 11, 12, 13, 14, 15))
+PLANE = frozenset(2 * g + 1 for g in (3, 5, 7, 9, 11, 12, 13, 14, 15))
+WORD = tuple(m for m in range(NM) if m not in PLANE)
+ND = 2
 
 
 def tile_ropemaskedattentionhead_pa_t_kernel(tc, x_bytes, x_scale, w_q, w_k, w_v, out_0, out_1, out_2):
     nc = tc.nc
     with ExitStack() as ctx:
         const = ctx.enter_context(tc.tile_pool(name="const", bufs=1))
-        work = ctx.enter_context(tc.tile_pool(name="work", bufs=3))
+        work = ctx.enter_context(tc.tile_pool(name="work", bufs=4))
         ps_t = ctx.enter_context(tc.psum_pool(name="ps_t", bufs=2))
         ps_y = ctx.enter_context(tc.psum_pool(name="ps_y", bufs=1))
         ps_r = ctx.enter_context(tc.psum_pool(name="ps_r", bufs=4))
@@ -91,72 +94,65 @@ def tile_ropemaskedattentionhead_pa_t_kernel(tc, x_bytes, x_scale, w_q, w_k, w_v
                                    in_=xb[:, n * XW + c * step:n * XW + (c + 1) * step].bitcast(FP8))
             st[("xbf", n)] = xbf
 
-        def turn(n):
-            words = st[("xbf", n)][:].bitcast(F32)
-            for h in range(1 if n in YSET else 2):
-                tp = ps_t.tile([P, 512], F32, name="tp", tag="tp")
-                for a2 in range(2):
-                    a = 2 * h + a2
-                    for u in range(2):
-                        nc.tensor.transpose(tp[:, u * 256 + a2 * P:u * 256 + (a2 + 1) * P],
-                                            words[:, 256 * a + u:256 * (a + 1):2], ident[:])
-                st[("tp", n, h)] = tp
+        def turn(m):
+            words = st[("xbf", m // 2)][:].bitcast(F32)
+            tp = ps_t.tile([P, 512], F32, name="tp", tag="tp")
+            for a2 in range(2):
+                a = 2 * (m % 2) + a2
+                for u in range(2):
+                    nc.tensor.transpose(tp[:, u * 256 + a2 * P:u * 256 + (a2 + 1) * P],
+                                        words[:, 256 * a + u:256 * (a + 1):2], ident[:])
+            st[("tp", m)] = tp
 
-        def turn_y(n):
-            xbf = st[("xbf", n)]
+        def turn_y(m):
+            xbf = st[("xbf", m // 2)]
             tpb = ps_y.tile([P, 1024], BF16, name="tpb", tag="tpb")
             for a2 in range(2):
-                a = 2 + a2
+                a = 2 * (m % 2) + a2
                 for t in range(4):
                     nc.tensor.transpose(tpb[:, t * 256 + a2 * P:t * 256 + (a2 + 1) * P],
                                         xbf[:, a * D + t:(a + 1) * D:4], ident_b[:])
             pl = work.tile([P, 4, 256], BF16, name="pl", tag="pl")
             for t in range(4):
                 nc.scalar.activation(out=pl[:, t, :], in_=tpb[:, t * 256:(t + 1) * 256], func=ACT.Copy, scale=sc4[:, t:t + 1])
-            st[("pl", n)] = pl
+            st[("pl", m)] = pl
 
-        def weave(n):
-            nc.scalar.copy(out=st[("grp", n)][:, 1024:2048].rearrange("p (c i t) -> p c t i", i=4, t=4),
-                           in_=st[("pl", n)][:].rearrange("p t (c i) -> p c t i", i=4))
+        def new_grp(m):
+            st[("grp", m)] = work.tile([P, 2 * P * 4], BF16, name="grp", tag="grp", align_bytes=64)
+            return st[("grp", m)]
 
-        def x_side(n):
-            scale_out(n, 0)
-            if n in YSET:
-                weave(n)
-            else:
-                scale_out(n, 1)
+        def weave(m):
+            nc.scalar.copy(out=new_grp(m)[:].rearrange("p (c i t) -> p c t i", i=4, t=4),
+                           in_=st[("pl", m)][:].rearrange("p t (c i) -> p c t i", i=4))
 
-        def turns_of(n):
-            turn(n)
-            if n in YSET:
-                turn_y(n)
-
-        def scale_out(n, h):
-            if h == 0:
-                st[("grp", n)] = work.tile([P, GT * P * 4], BF16, name="grp", tag="grp", align_bytes=64)
-            grp = st[("grp", n)]
+        def scale_out(m):
             nc.vector.tensor_tensor(
-                out=grp[:, h * 1024:(h + 1) * 1024].rearrange("p (r u e) -> p r u e", u=2, e=2),
-                in0=st[("tp", n, h)][:].bitcast(BF16).rearrange("p (u r e) -> p r u e", u=2, e=2),
+                out=new_grp(m)[:].rearrange("p (r u e) -> p r u e", u=2, e=2),
+                in0=st[("tp", m)][:].bitcast(BF16).rearrange("p (u r e) -> p r u e", u=2, e=2),
                 in1=sc4[:].rearrange("p (u e) -> p u e", u=2).unsqueeze(1).to_broadcast([P, 256, 2, 2]),
                 op=ALU.mult)
 
-        def quant(n):
-            codes = work.tile([P, GT * P], U32, name="codes", tag="codes", align_bytes=64)
-            xs = work.tile([P, GT * P], U8, name="xs", tag="xs", align_bytes=64)
-            nc.vector.quantize_mx(out=codes[:].bitcast(FP8X4), scales=xs[:], in_=st[("grp", n)][:])
-            st[("codes", n)] = codes
-            st[("xs", n)] = xs
+        def quant(m):
+            codes = work.tile([P, 2 * P], U32, name="codes", tag="codes", align_bytes=64)
+            xs = work.tile([P, 2 * P], U8, name="xs", tag="xs", align_bytes=64)
+            nc.vector.quantize_mx(out=codes[:].bitcast(FP8X4), scales=xs[:], in_=st[("grp", m)][:])
+            st[("codes", m)] = codes
+            st[("xs", m)] = xs
 
-        def mult(n):
-            codes, xs = st[("codes", n)], st[("xs", n)]
-            vb = ps_v.tile([P, GT * HD], F32, name="vb", tag="vb")
-            st[("vb", n)] = vb
-            for a in range(GT):
-                mm = ps_r.tile([P, 384], F32, name="mm", tag="mm")
-                st[("mm", n, a)] = mm
-                lt = codes[:, a * P:(a + 1) * P].bitcast(FP8X4)
-                ls = xs[:, a * P:(a + 1) * P]
+        def mult(m):
+            codes, xs = st[("codes", m)], st[("xs", m)]
+            if m % 2 == 0:
+                st[("vb", m // 2)] = ps_v.tile([P, GT * HD], F32, name="vb", tag="vb")
+            vb = st[("vb", m // 2)]
+            for a2 in range(2):
+                a = 2 * (m % 2) + a2
+                mm = ps_r.tile([P, 512], F32, name="mm", tag="mm")
+                st[("mm", m, a2)] = mm
+                lt = codes[:, a2 * P:(a2 + 1) * P].bitcast(FP8X4)
+                ls = xs[:, a2 * P:(a2 + 1) * P]
+                for r in range(ND):
+                    nc.tensor.matmul_mx(out=mm[:, 384:512], lhsT=lt, lhsT_scale=ls, rhs=wc[:, 256:384].bitcast(FP8X4),
+                                        rhs_scale=ws[:, 256:384], start=True, stop=True)
                 nc.tensor.matmul_mx(out=mm[:, 0:256], lhsT=lt, lhsT_scale=ls, rhs=wc[:, 0:256].bitcast(FP8X4),
                                     rhs_scale=ws[:, 0:256], start=True, stop=True)
                 nc.tensor.matmul_mx(out=mm[:, 256:384], lhsT=lt, lhsT_scale=ls, rhs=wc[:, 0:128].bitcast(FP8X4),
@@ -166,40 +162,42 @@ def tile_ropemaskedattentionhead_pa_t_kernel(tc, x_bytes, x_scale, w_q, w_k, w_v
                 nc.tensor.matmul_mx(out=vb[:, a * HD:(a + 1) * HD], lhsT=lt, lhsT_scale=ls,
                                     rhs=wc[:, 256:384].bitcast(FP8X4), rhs_scale=ws[:, 256:384], start=True, stop=True)
 
-        def rope(n, a):
-            if a == 0:
-                st[("prod", n)] = work.tile([P, GT, 2, 3, HALF], F32, name="prod", tag="prod")
-            prod = st[("prod", n)]
-            i = (n % (NI // GT)) * GT + a
+        def rope(m, a2):
+            if a2 == 0:
+                st[("prod", m)] = work.tile([P, 2, 2, 3, HALF], F32, name="prod", tag="prod")
+            prod = st[("prod", m)]
+            i = ((m // 2) % (NI // GT)) * GT + 2 * (m % 2) + a2
             nc.vector.tensor_tensor(
-                out=prod[:, a, :, :, :].rearrange("p w c j -> p c w j"),
-                in0=st[("mm", n, a)][:].rearrange("p (c w j) -> p c w j", c=3, w=2),
+                out=prod[:, a2, :, :, :].rearrange("p w c j -> p c w j"),
+                in0=st[("mm", m, a2)][:, 0:384].rearrange("p (c w j) -> p c w j", c=3, w=2),
                 in1=tab[:, i, :, :].unsqueeze(2).to_broadcast([P, 3, 2, HALF]),
                 op=ALU.mult)
 
-        def add_up(n, a0, a1, w0, w1, eng):
-            if a0 == 0 and w0 == 0:
+        def add_up(m, eng):
+            n, h = divmod(m, 2)
+            if h == 0:
                 st[("o_r", n)] = work.tile([P, 2, GT * HD], F32, name="o_r", tag="o_r")
             b, g = divmod(n, NI // GT)
-            o_r, prod = st[("o_r", n)], st[("prod", n)]
+            o_r, prod = st[("o_r", n)], st[("prod", m)]
+            a0, a1 = 2 * h, 2 * h + 2
             eng.tensor_tensor(
-                out=o_r[:, w0:w1, a0 * HD:a1 * HD].rearrange("p w (a h j) -> p a w h j", h=2, j=HALF),
-                in0=prod[:, a0:a1, w0:w1, 0:2, :],
-                in1=prod[:, a0:a1, w0:w1, 2:3, :].to_broadcast([P, a1 - a0, w1 - w0, 2, HALF]), op=ALU.add)
-            for w in range(w0, w1):
-                nc.sync.dma_start(out=o_views[w][b][:, (g * GT + a0) * HD:(g * GT + a1) * HD], in_=o_r[:, w, a0 * HD:a1 * HD])
+                out=o_r[:, :, a0 * HD:a1 * HD].rearrange("p w (a h j) -> p a w h j", h=2, j=HALF),
+                in0=prod[:, :, :, 0:2, :],
+                in1=prod[:, :, :, 2:3, :].to_broadcast([P, 2, 2, 2, HALF]), op=ALU.add)
+            if n + 1 == NG:
+                s0, s1 = a0, a1
+            elif h == 1:
+                s0, s1 = 0, GT
+            else:
+                return
+            for w in range(2):
+                nc.sync.dma_start(out=o_views[w][b][:, (g * GT + s0) * HD:(g * GT + s1) * HD], in_=o_r[:, w, s0 * HD:s1 * HD])
 
         def finish_v(n):
             b, g = divmod(n, NI // GT)
             o_v = work.tile([P, GT * HD], F32, name="o_v", tag="o_v")
             nc.scalar.copy(out=o_v[:], in_=st[("vb", n)][:])
             nc.sync.dma_start(out=o_views[2][b][:, g * GT * HD:(g + 1) * GT * HD], in_=o_v[:])
-
-        def idle(n):
-            dm = ps_v.tile([P, GT * HD], F32, name="dm", tag="vb")
-            for r in range(2):
-                nc.tensor.matmul_mx(out=dm[:], lhsT=wc[:, 0:128].bitcast(FP8X4), lhsT_scale=ws[:, 0:128],
-                                    rhs=st[("codes", n)][:].bitcast(FP8X4), rhs_scale=st[("xs", n)][:], start=True, stop=True)
 
         def table(c):
             rows = slice(c * GT, (c + 1) * GT)
@@ -243,50 +241,41 @@ def tile_ropemaskedattentionhead_pa_t_kernel(tc, x_bytes, x_scale, w_q, w_k, w_v
         for u in range(2):
             nc.tensor.transpose(tw2[:, u * P:(u + 1) * P], w_c[:].bitcast(F32)[:, u:256:2], ident[:])
         cast(0, 2)
-        turns_of(0)
+        turn(WORD[0])
+        turn(WORD[1])
         nc.vector.tensor_copy(out=wg_ab[:].bitcast(F32).rearrange("p (r u) -> p r u", u=2),
                               in_=tw[:].rearrange("p (u r) -> p r u", u=2))
         nc.vector.tensor_copy(out=wg_c[:].bitcast(F32).rearrange("p (r u) -> p r u", u=2),
                               in_=tw2[:, 0:256].rearrange("p (u r) -> p r u", u=2))
         table(0)
-        scale_out(0, 0)
         cast(1, 2)
-        nc.vector.quantize_mx(out=wc[:, 0:256].bitcast(FP8X4), scales=ws[:, 0:256], in_=wg_ab[:])
-        scale_out(0, 1)
-        nc.vector.quantize_mx(out=wc[:, 256:384].bitcast(FP8X4), scales=ws[:, 256:384], in_=wg_c[:])
-        turns_of(1)
-        quant(0)
-        mult(0)
-        table(1)
-        cast(2, 1)
-        x_side(1)
-        turns_of(2)
-        cast(3, 1)
 
         with tc.manual_schedule(engines={mybir.EngineType.DVE}):
-            for n in range(NG):
-                last = n + 1 == NG
-                finish_v(n)
-                if not last:
-                    idle(n)
-                rope(n, 0)
-                rope(n, 1)
-                if last:
-                    add_up(n, 0, 2, 0, 2, nc.gpsimd)
-                rope(n, 2)
-                rope(n, 3)
-                if last:
-                    add_up(n, 2, 4, 0, 2, nc.vector)
-                else:
-                    add_up(n, 0, 4, 0, 1, nc.gpsimd)
-                    add_up(n, 0, 4, 1, 2, nc.gpsimd)
-                    quant(n + 1)
-                    mult(n + 1)
-                if n + 2 < NG:
-                    x_side(n + 2)
-                if n + 3 < NG:
-                    turns_of(n + 3)
-                if n + 2 < NI // GT:
-                    table(n + 2)
-                if n + 4 < NG:
-                    cast(n + 4, 1)
+            for m in range(-6, NM):
+                if m >= 0 and m % 2 == 0:
+                    finish_v(m // 2)
+                if m >= 0:
+                    rope(m, 0)
+                    rope(m, 1)
+                    add_up(m, nc.vector if m + 1 == NM else nc.gpsimd)
+                if 0 <= m + 3 < NM:
+                    quant(m + 3)
+                if 0 <= m + 2 < NM:
+                    mult(m + 2)
+                if m + 5 in PLANE:
+                    weave(m + 5)
+                if m + 4 in WORD:
+                    scale_out(m + 4)
+                    k = WORD.index(m + 4) + 2
+                    if k < len(WORD):
+                        turn(WORD[k])
+                if m + 4 == 0:
+                    nc.vector.quantize_mx(out=wc[:, 0:256].bitcast(FP8X4), scales=ws[:, 0:256], in_=wg_ab[:])
+                    nc.vector.quantize_mx(out=wc[:, 256:384].bitcast(FP8X4), scales=ws[:, 256:384], in_=wg_c[:])
+                if m + 7 in PLANE:
+                    turn_y(m + 7)
+                if m % 2 == 0:
+                    if 1 <= m // 2 + 3 < NI // GT:
+                        table(m // 2 + 3)
+                    if 2 <= m // 2 + 5 < NG:
+                        cast(m // 2 + 5, 1)

@@ -202,12 +202,11 @@ def tile_ropemaskedattentionhead_pa_t_kernel(tc, x_bytes, x_scale, w_q, w_k, w_v
         def table(c):
             rows = slice(c * GT, (c + 1) * GT)
             nc.scalar.activation(out=sin_t[:, rows, :], in_=frac[:, rows, :], func=ACT.Sin, scale=2.0 * PI)
-            nc.scalar.activation(out=half_t[:, rows, :], in_=frac[:, rows, :], func=ACT.Sin, scale=PI)
-            nc.gpsimd.tensor_tensor(out=sq_t[:, rows, :], in0=half_t[:, rows, :], in1=half_t[:, rows, :], op=ALU.mult)
-            nc.gpsimd.tensor_scalar(out=ncos_t[:, rows, :], in0=sq_t[:, rows, :], scalar1=2.0, scalar2=-1.0, op0=ALU.mult, op1=ALU.add)
-            nc.gpsimd.tensor_scalar(out=tab[:, rows, 2, :], in0=sq_t[:, rows, :], scalar1=-2.0, scalar2=1.0, op0=ALU.mult, op1=ALU.add)
-            nc.gpsimd.tensor_tensor(out=tab[:, rows, 0, :], in0=ncos_t[:, rows, :], in1=sin_t[:, rows, :], op=ALU.subtract)
-            nc.gpsimd.tensor_tensor(out=tab[:, rows, 1, :], in0=ncos_t[:, rows, :], in1=sin_t[:, rows, :], op=ALU.add)
+            nc.scalar.activation(out=nsin_t[:, rows, :], in_=frac[:, rows, :], func=ACT.Sin, scale=-2.0 * PI)
+            nc.scalar.activation(out=absf[:, rows, :], in_=frac[:, rows, :], func=ACT.Abs)
+            nc.scalar.activation(out=tab[:, rows, 2, :], in_=absf[:, rows, :], func=ACT.Sin, scale=-2.0 * PI, bias=0.5 * PI)
+            nc.gpsimd.tensor_tensor(out=tab[:, rows, 1, :], in0=sin_t[:, rows, :], in1=tab[:, rows, 2, :], op=ALU.subtract)
+            nc.gpsimd.tensor_tensor(out=tab[:, rows, 0, :], in0=nsin_t[:, rows, :], in1=tab[:, rows, 2, :], op=ALU.subtract)
 
         pos = const.tile([P, NI], F32, name="pos")
         nc.vector.tensor_copy(out=pos[:], in_=idx_i[:])
@@ -224,9 +223,8 @@ def tile_ropemaskedattentionhead_pa_t_kernel(tc, x_bytes, x_scale, w_q, w_k, w_v
         frac = const.tile([P, NI, HALF], F32, name="frac")
         nc.vector.tensor_tensor(out=frac[:], in0=ang[:], in1=whole[:], op=ALU.subtract)
         sin_t = const.tile([P, NI, HALF], F32, name="sin_t")
-        half_t = const.tile([P, NI, HALF], F32, name="half_t")
-        sq_t = const.tile([P, NI, HALF], F32, name="sq_t")
-        ncos_t = const.tile([P, NI, HALF], F32, name="ncos_t")
+        nsin_t = const.tile([P, NI, HALF], F32, name="nsin_t")
+        absf = const.tile([P, NI, HALF], F32, name="absf")
         tab = const.tile([P, NI, 3, HALF], F32, name="tab")
 
         wc = const.tile([P, 384], U32, name="wc", align_bytes=64)

@@ -125,11 +125,12 @@ def tile_ropemaskedattentionhead_pa_t_kernel(tc, x_bytes, x_scale, w_q, w_k, w_v
             nc.scalar.copy(out=new_grp(m)[:].rearrange("p (c i t) -> p c t i", i=4, t=4),
                            in_=st[("pl", m)][:].rearrange("p t (c i) -> p c t i", i=4))
 
-        def scale_out(m):
+        def scale_out(m, r0, r1):
+            grp = new_grp(m) if r0 == 0 else st[("grp", m)]
             nc.vector.tensor_tensor(
-                out=new_grp(m)[:].rearrange("p (r u e) -> p r u e", u=2, e=2),
-                in0=st[("tp", m)][:].bitcast(BF16).rearrange("p (u r e) -> p r u e", u=2, e=2),
-                in1=sc4[:].rearrange("p (u e) -> p u e", u=2).unsqueeze(1).to_broadcast([P, 256, 2, 2]),
+                out=grp[:, 4 * r0:4 * r1].rearrange("p (r u e) -> p r u e", u=2, e=2),
+                in0=st[("tp", m)][:].bitcast(BF16).rearrange("p (u r e) -> p r u e", u=2, e=2)[:, r0:r1, :, :],
+                in1=sc4[:].rearrange("p (u e) -> p u e", u=2).unsqueeze(1).to_broadcast([P, r1 - r0, 2, 2]),
                 op=ALU.mult)
 
         def quant(m):
@@ -263,10 +264,12 @@ def tile_ropemaskedattentionhead_pa_t_kernel(tc, x_bytes, x_scale, w_q, w_k, w_v
                 if m + 5 in PLANE:
                     weave(m + 5)
                 if m + 4 in WORD:
-                    scale_out(m + 4)
+                    scale_out(m + 4, P if m + 3 in PLANE else 0, 2 * P)
                     k = WORD.index(m + 4) + 2
                     if k < len(WORD):
                         turn(WORD[k])
+                elif m + 4 in PLANE and m + 5 < NM:
+                    scale_out(m + 5, 0, P)
                 if m + 4 == 0:
                     nc.vector.quantize_mx(out=wc[:, 0:256].bitcast(FP8X4), scales=ws[:, 0:256], in_=wg_ab[:])
                     nc.vector.quantize_mx(out=wc[:, 256:384].bitcast(FP8X4), scales=ws[:, 256:384], in_=wg_c[:])

@@ -28,7 +28,7 @@ MAGIC = 8388608.0
 VCAST = frozenset((0,))
 PLANE = frozenset(2 * g + 1 for g in (3, 5, 7, 9, 11, 12, 13, 14, 15))
 WORD = tuple(m for m in range(NM) if m not in PLANE)
-ND = 2
+ND = 1
 
 
 def tile_ropemaskedattentionhead_pa_t_kernel(tc, x_bytes, x_scale, w_q, w_k, w_v, out_0, out_1, out_2):

@@ -28,7 +28,7 @@ MAGIC = 8388608.0
 VCAST = frozenset((0,))
 PLANE = frozenset(2 * g + 1 for g in (3, 5, 7, 9, 11, 12, 13, 14, 15))
 WORD = tuple(m for m in range(NM) if m not in PLANE)
-ND = 1
+ND = 0
 
 
 def tile_ropemaskedattentionhead_pa_t_kernel(tc, x_bytes, x_scale, w_q, w_k, w_v, out_0, out_1, out_2):

@@ -256,7 +256,11 @@ def tile_ropemaskedattentionhead_pa_t_kernel(tc, x_bytes, x_scale, w_q, w_k, w_v
                 if m >= 0:
                     rope(m, 0)
                     rope(m, 1)
-                    add_up(m, nc.vector if m + 1 == NM else nc.gpsimd)
+                    if m + 2 < NM:
+                        add_up(m, nc.gpsimd)
+                    elif m + 1 == NM:
+                        add_up(m - 1, nc.vector)
+                        add_up(m, nc.vector)
                 if 0 <= m + 3 < NM:
                     quant(m + 3)
                 if 0 <= m + 2 < NM:

@@ -59,14 +59,15 @@ def tile_ropemaskedattentionhead_pa_t_kernel(tc, x_bytes, x_scale, w_q, w_k, w_v
         w_b = const.tile([P, D], BF16, name="w_b")
         w_c = const.tile([P, D], BF16, name="w_c")
         sc4 = const.tile([P, 4], F32, name="sc4")
+        with nc.allow_non_contiguous_dma(reason="four scales to a partition"):
+            nc.sync.dma_start(out=sc4[:], in_=x_scale.rearrange("a b (p t) -> p (a b t)", t=4))
+        load(1, 1)
         nc.sync.dma_start(out=w_a[0:HALF, :], in_=w_q[HALF:HD, :])
         nc.sync.dma_start(out=w_a[HALF:P, :], in_=w_k[HALF:HD, :])
         nc.sync.dma_start(out=w_b[0:HALF, :], in_=w_q[0:HALF, :])
         nc.sync.dma_start(out=w_b[HALF:P, :], in_=w_k[0:HALF, :])
         nc.sync.dma_start(out=w_c[:], in_=w_v[:, :])
-        with nc.allow_non_contiguous_dma(reason="four scales to a partition"):
-            nc.sync.dma_start(out=sc4[:], in_=x_scale.rearrange("a b (p t) -> p (a b t)", t=4))
-        for n in range(1, NG):
+        for n in range(2, NG):
             load(n, 1)
 
         idx_i = const.tile([P, NI], I32, name="idx_i")
@@ -232,6 +233,9 @@ def tile_ropemaskedattentionhead_pa_t_kernel(tc, x_bytes, x_scale, w_q, w_k, w_v
         ws = const.tile([P, 384], U8, name="ws", align_bytes=64)
         wg_ab = const.tile([P, 1024], BF16, name="wg_ab", align_bytes=64)
         wg_c = const.tile([P, 512], BF16, name="wg_c", align_bytes=64)
+        cast(0, 2)
+        turn(WORD[0])
+        turn(WORD[1])
         tw = ps_r.tile([P, 512], F32, name="tw", tag="mm")
         for a2, w_t in enumerate((w_a, w_b)):
             for u in range(2):
@@ -239,13 +243,6 @@ def tile_ropemaskedattentionhead_pa_t_kernel(tc, x_bytes, x_scale, w_q, w_k, w_v
         tw2 = ps_r.tile([P, 512], F32, name="tw2", tag="mm")
         for u in range(2):
             nc.tensor.transpose(tw2[:, u * P:(u + 1) * P], w_c[:].bitcast(F32)[:, u:256:2], ident[:])
-        cast(0, 2)
-        turn(WORD[0])
-        turn(WORD[1])
-        nc.vector.tensor_copy(out=wg_ab[:].bitcast(F32).rearrange("p (r u) -> p r u", u=2),
-                              in_=tw[:].rearrange("p (u r) -> p r u", u=2))
-        nc.vector.tensor_copy(out=wg_c[:].bitcast(F32).rearrange("p (r u) -> p r u", u=2),
-                              in_=tw2[:, 0:256].rearrange("p (u r) -> p r u", u=2))
         table(0)
         cast(1, 2)
 
@@ -275,6 +272,11 @@ def tile_ropemaskedattentionhead_pa_t_kernel(tc, x_bytes, x_scale, w_q, w_k, w_v
                 elif m + 4 in PLANE and m + 5 < NM:
                     scale_out(m + 5, 0, P)
                 if m + 4 == 0:
+                    nc.vector.tensor_copy(out=wg_ab[:].bitcast(F32).rearrange("p (r u) -> p r u", u=2),
+                                          in_=tw[:].rearrange("p (u r) -> p r u", u=2))
+                    nc.vector.tensor_copy(out=wg_c[:].bitcast(F32).rearrange("p (r u) -> p r u", u=2),
+                                          in_=tw2[:, 0:256].rearrange("p (u r) -> p r u", u=2))
+                if m + 4 == 1:
                     nc.vector.quantize_mx(out=wc[:, 0:256].bitcast(FP8X4), scales=ws[:, 0:256], in_=wg_ab[:])
                     nc.vector.quantize_mx(out=wc[:, 256:384].bitcast(FP8X4), scales=ws[:, 256:384], in_=wg_c[:])
                 if m + 7 in PLANE:

@@ -26,7 +26,7 @@ PI = 3.141592653589793
 RATIO = 10000.0 ** (-1.0 / HALF)
 MAGIC = 8388608.0
 VCAST = frozenset((0,))
-PLANE = frozenset(2 * g + 1 for g in (3, 5, 7, 9, 11, 12, 13, 14, 15))
+PLANE = frozenset(2 * g + 1 for g in (3, 5, 7, 9, 10, 11, 12, 13, 14, 15))
 WORD = tuple(m for m in range(NM) if m not in PLANE)
 ND = 0
 

@@ -26,9 +26,8 @@ PI = 3.141592653589793
 RATIO = 10000.0 ** (-1.0 / HALF)
 MAGIC = 8388608.0
 VCAST = frozenset((0,))
-PLANE = frozenset(2 * g + 1 for g in (3, 5, 7, 9, 10, 11, 12, 13, 14, 15))
+PLANE = frozenset(2 * g + 1 for g in range(2, NG))
 WORD = tuple(m for m in range(NM) if m not in PLANE)
-ND = 0
 
 
 def tile_ropemaskedattentionhead_pa_t_kernel(tc, x_bytes, x_scale, w_q, w_k, w_v, out_0, out_1, out_2):
@@ -143,26 +142,27 @@ def tile_ropemaskedattentionhead_pa_t_kernel(tc, x_bytes, x_scale, w_q, w_k, w_v
 
         def mult(m):
             codes, xs = st[("codes", m)], st[("xs", m)]
-            if m % 2 == 0:
-                st[("vb", m // 2)] = ps_v.tile([P, GT * HD], F32, name="vb", tag="vb")
-            vb = st[("vb", m // 2)]
             for a2 in range(2):
-                a = 2 * (m % 2) + a2
                 mm = ps_r.tile([P, 512], F32, name="mm", tag="mm")
                 st[("mm", m, a2)] = mm
                 lt = codes[:, a2 * P:(a2 + 1) * P].bitcast(FP8X4)
                 ls = xs[:, a2 * P:(a2 + 1) * P]
-                for r in range(ND):
-                    nc.tensor.matmul_mx(out=mm[:, 384:512], lhsT=lt, lhsT_scale=ls, rhs=wc[:, 256:384].bitcast(FP8X4),
-                                        rhs_scale=ws[:, 256:384], start=True, stop=True)
                 nc.tensor.matmul_mx(out=mm[:, 0:256], lhsT=lt, lhsT_scale=ls, rhs=wc[:, 0:256].bitcast(FP8X4),
                                     rhs_scale=ws[:, 0:256], start=True, stop=True)
                 nc.tensor.matmul_mx(out=mm[:, 256:384], lhsT=lt, lhsT_scale=ls, rhs=wc[:, 0:128].bitcast(FP8X4),
                                     rhs_scale=ws[:, 0:128], start=True, stop=False)
                 nc.tensor.matmul_mx(out=mm[:, 256:384], lhsT=lt, lhsT_scale=ls, rhs=wc[:, 128:256].bitcast(FP8X4),
                                     rhs_scale=ws[:, 128:256], start=False, stop=True)
-                nc.tensor.matmul_mx(out=vb[:, a * HD:(a + 1) * HD], lhsT=lt, lhsT_scale=ls,
+
+        def mult_v(n):
+            vb = ps_v.tile([P, GT * HD], F32, name="vb", tag="vb")
+            for a in range(GT):
+                m, a2 = 2 * n + a // 2, a % 2
+                nc.tensor.matmul_mx(out=vb[:, a * HD:(a + 1) * HD],
+                                    lhsT=st[("codes", m)][:, a2 * P:(a2 + 1) * P].bitcast(FP8X4),
+                                    lhsT_scale=st[("xs", m)][:, a2 * P:(a2 + 1) * P],
                                     rhs=wc[:, 256:384].bitcast(FP8X4), rhs_scale=ws[:, 256:384], start=True, stop=True)
+            st[("vb", n)] = vb
 
         def rope(m, a2):
             if a2 == 0:
@@ -262,6 +262,8 @@ def tile_ropemaskedattentionhead_pa_t_kernel(tc, x_bytes, x_scale, w_q, w_k, w_v
                     quant(m + 3)
                 if 0 <= m + 2 < NM:
                     mult(m + 2)
+                    if m % 2 == 1:
+                        mult_v((m + 2) // 2)
                 if m + 5 in PLANE:
                     weave(m + 5)
                 if m + 4 in WORD:

@@ -25,8 +25,7 @@ NM = 2 * NG
 PI = 3.141592653589793
 RATIO = 10000.0 ** (-1.0 / HALF)
 MAGIC = 8388608.0
-VCAST = frozenset((0,))
-PLANE = frozenset(2 * g + 1 for g in range(2, NG))
+PLANE = frozenset(2 * g + 1 for g in range(2, NG) if g % 4 != 0)
 WORD = tuple(m for m in range(NM) if m not in PLANE)
 
 
@@ -83,15 +82,11 @@ def tile_ropemaskedattentionhead_pa_t_kernel(tc, x_bytes, x_scale, w_q, w_k, w_v
         st = {}
 
         def cast(n, pieces):
-            xbf = work.tile([P, XW], BF16, name="xbf", tag="xbf")
+            xbf = work.tile([P, XW], BF16, name="xbf", tag="xbf", bufs=6)
             step = XW // pieces
             for c in range(pieces):
-                if n in VCAST:
-                    nc.vector.tensor_copy(out=xbf[:, c * step:(c + 1) * step],
-                                          in_=xb[:, n * XW + c * step:n * XW + (c + 1) * step].bitcast(FP8))
-                else:
-                    nc.scalar.copy(out=xbf[:, c * step:(c + 1) * step],
-                                   in_=xb[:, n * XW + c * step:n * XW + (c + 1) * step].bitcast(FP8))
+                nc.scalar.copy(out=xbf[:, c * step:(c + 1) * step],
+                               in_=xb[:, n * XW + c * step:n * XW + (c + 1) * step].bitcast(FP8))
             st[("xbf", n)] = xbf
 
         def turn(m):
@@ -134,8 +129,8 @@ def tile_ropemaskedattentionhead_pa_t_kernel(tc, x_bytes, x_scale, w_q, w_k, w_v
                 op=ALU.mult)
 
         def quant(m):
-            codes = work.tile([P, 2 * P], U32, name="codes", tag="codes", align_bytes=64)
-            xs = work.tile([P, 2 * P], U8, name="xs", tag="xs", align_bytes=64)
+            codes = work.tile([P, 2 * P], U32, name="codes", tag="codes", align_bytes=64, bufs=6)
+            xs = work.tile([P, 2 * P], U8, name="xs", tag="xs", align_bytes=64, bufs=6)
             nc.vector.quantize_mx(out=codes[:].bitcast(FP8X4), scales=xs[:], in_=st[("grp", m)][:])
             st[("codes", m)] = codes
             st[("xs", m)] = xs
@@ -210,6 +205,7 @@ def tile_ropemaskedattentionhead_pa_t_kernel(tc, x_bytes, x_scale, w_q, w_k, w_v
             nc.gpsimd.tensor_tensor(out=tab[:, rows, 1, :], in0=sin_t[:, rows, :], in1=tab[:, rows, 2, :], op=ALU.subtract)
             nc.gpsimd.tensor_tensor(out=tab[:, rows, 0, :], in0=nsin_t[:, rows, :], in1=tab[:, rows, 2, :], op=ALU.subtract)
 
+        ctx.enter_context(tc.manual_schedule(engines={mybir.EngineType.DVE, mybir.EngineType.Activation}))
         pos = const.tile([P, NI], F32, name="pos")
         nc.vector.tensor_copy(out=pos[:], in_=idx_i[:])
         turns = const.tile([P, HALF], F32, name="turns")
@@ -243,48 +239,45 @@ def tile_ropemaskedattentionhead_pa_t_kernel(tc, x_bytes, x_scale, w_q, w_k, w_v
         tw2 = ps_r.tile([P, 512], F32, name="tw2", tag="mm")
         for u in range(2):
             nc.tensor.transpose(tw2[:, u * P:(u + 1) * P], w_c[:].bitcast(F32)[:, u:256:2], ident[:])
-        table(0)
         cast(1, 2)
+        for c in range(NI // GT):
+            table(c)
 
-        with tc.manual_schedule(engines={mybir.EngineType.DVE}):
-            for m in range(-6, NM):
-                if m >= 0 and m % 2 == 0:
-                    finish_v(m // 2)
-                if m >= 0:
-                    rope(m, 0)
-                    rope(m, 1)
-                    if m + 2 < NM:
-                        add_up(m, nc.gpsimd)
-                    elif m + 1 == NM:
-                        add_up(m - 1, nc.vector)
-                        add_up(m, nc.vector)
-                if 0 <= m + 3 < NM:
-                    quant(m + 3)
-                if 0 <= m + 2 < NM:
-                    mult(m + 2)
-                    if m % 2 == 1:
-                        mult_v((m + 2) // 2)
-                if m + 5 in PLANE:
-                    weave(m + 5)
-                if m + 4 in WORD:
-                    scale_out(m + 4, P if m + 3 in PLANE else 0, 2 * P)
-                    k = WORD.index(m + 4) + 2
-                    if k < len(WORD):
-                        turn(WORD[k])
-                elif m + 4 in PLANE and m + 5 < NM:
-                    scale_out(m + 5, 0, P)
-                if m + 4 == 0:
-                    nc.vector.tensor_copy(out=wg_ab[:].bitcast(F32).rearrange("p (r u) -> p r u", u=2),
-                                          in_=tw[:].rearrange("p (u r) -> p r u", u=2))
-                    nc.vector.tensor_copy(out=wg_c[:].bitcast(F32).rearrange("p (r u) -> p r u", u=2),
-                                          in_=tw2[:, 0:256].rearrange("p (u r) -> p r u", u=2))
-                if m + 4 == 1:
-                    nc.vector.quantize_mx(out=wc[:, 0:256].bitcast(FP8X4), scales=ws[:, 0:256], in_=wg_ab[:])
-                    nc.vector.quantize_mx(out=wc[:, 256:384].bitcast(FP8X4), scales=ws[:, 256:384], in_=wg_c[:])
-                if m + 7 in PLANE:
-                    turn_y(m + 7)
-                if m % 2 == 0:
-                    if 1 <= m // 2 + 3 < NI // GT:
-                        table(m // 2 + 3)
-                    if 2 <= m // 2 + 5 < NG:
-                        cast(m // 2 + 5, 1)
+        for m in range(-6, NM):
+            if m >= 0 and m % 2 == 0:
+                finish_v(m // 2)
+            if m >= 0:
+                rope(m, 0)
+                rope(m, 1)
+                if m + 2 < NM:
+                    add_up(m, nc.gpsimd)
+                elif m + 1 == NM:
+                    add_up(m - 1, nc.vector)
+                    add_up(m, nc.vector)
+            if 0 <= m + 3 < NM:
+                quant(m + 3)
+            if 0 <= m + 2 < NM:
+                mult(m + 2)
+                if m % 2 == 1:
+                    mult_v((m + 2) // 2)
+            if m + 6 in PLANE:
+                weave(m + 6)
+            if m % 2 == 0 and 2 <= m // 2 + 5 < NG:
+                cast(m // 2 + 5, 1)
+            if m + 8 in PLANE:
+                turn_y(m + 8)
+            if m + 4 in WORD:
+                scale_out(m + 4, P if m + 3 in PLANE else 0, 2 * P)
+                k = WORD.index(m + 4) + 2
+                if k < len(WORD):
+                    turn(WORD[k])
+            elif m + 4 in PLANE and m + 5 < NM:
+                scale_out(m + 5, 0, P)
+            if m + 4 == 0:
+                nc.vector.tensor_copy(out=wg_ab[:].bitcast(F32).rearrange("p (r u) -> p r u", u=2),
+                                      in_=tw[:].rearrange("p (u r) -> p r u", u=2))
+                nc.vector.tensor_copy(out=wg_c[:].bitcast(F32).rearrange("p (r u) -> p r u", u=2),
+                                      in_=tw2[:, 0:256].rearrange("p (u r) -> p r u", u=2))
+            if m + 4 == 1:
+                nc.vector.quantize_mx(out=wc[:, 0:256].bitcast(FP8X4), scales=ws[:, 0:256], in_=wg_ab[:])
+                nc.vector.quantize_mx(out=wc[:, 256:384].bitcast(FP8X4), scales=ws[:, 256:384], in_=wg_c[:])

@@ -25,7 +25,7 @@ NM = 2 * NG
 PI = 3.141592653589793
 RATIO = 10000.0 ** (-1.0 / HALF)
 MAGIC = 8388608.0
-PLANE = frozenset(2 * g + 1 for g in range(2, NG) if g % 4 != 0)
+PLANE = frozenset(2 * g + 1 for g in range(2, NG) if g not in (6, 10))
 WORD = tuple(m for m in range(NM) if m not in PLANE)
 
 
@@ -60,10 +60,10 @@ def tile_ropemaskedattentionhead_pa_t_kernel(tc, x_bytes, x_scale, w_q, w_k, w_v
         with nc.allow_non_contiguous_dma(reason="four scales to a partition"):
             nc.sync.dma_start(out=sc4[:], in_=x_scale.rearrange("a b (p t) -> p (a b t)", t=4))
         load(1, 1)
-        nc.sync.dma_start(out=w_a[0:HALF, :], in_=w_q[HALF:HD, :])
-        nc.sync.dma_start(out=w_a[HALF:P, :], in_=w_k[HALF:HD, :])
-        nc.sync.dma_start(out=w_b[0:HALF, :], in_=w_q[0:HALF, :])
-        nc.sync.dma_start(out=w_b[HALF:P, :], in_=w_k[0:HALF, :])
+        nc.sync.dma_start(out=w_a[0:HALF, :], in_=w_q[0:HALF, :])
+        nc.sync.dma_start(out=w_a[HALF:P, :], in_=w_k[0:HALF, :])
+        nc.sync.dma_start(out=w_b[0:HALF, :], in_=w_q[HALF:HD, :])
+        nc.sync.dma_start(out=w_b[HALF:P, :], in_=w_k[HALF:HD, :])
         nc.sync.dma_start(out=w_c[:], in_=w_v[:, :])
         for n in range(2, NG):
             load(n, 1)
@@ -146,8 +146,8 @@ def tile_ropemaskedattentionhead_pa_t_kernel(tc, x_bytes, x_scale, w_q, w_k, w_v
                                     rhs_scale=ws[:, 0:256], start=True, stop=True)
                 nc.tensor.matmul_mx(out=mm[:, 256:384], lhsT=lt, lhsT_scale=ls, rhs=wc[:, 0:128].bitcast(FP8X4),
                                     rhs_scale=ws[:, 0:128], start=True, stop=False)
-                nc.tensor.matmul_mx(out=mm[:, 256:384], lhsT=lt, lhsT_scale=ls, rhs=wc[:, 128:256].bitcast(FP8X4),
-                                    rhs_scale=ws[:, 128:256], start=False, stop=True)
+                nc.tensor.matmul_mx(out=mm[:, 256:384], lhsT=lt, lhsT_scale=ls, rhs=wc[:, 384:512].bitcast(FP8X4),
+                                    rhs_scale=ws[:, 384:512], start=False, stop=True)
 
         def mult_v(n):
             vb = ps_v.tile([P, GT * HD], F32, name="vb", tag="vb")
@@ -198,14 +198,18 @@ def tile_ropemaskedattentionhead_pa_t_kernel(tc, x_bytes, x_scale, w_q, w_k, w_v
 
         def table(c):
             rows = slice(c * GT, (c + 1) * GT)
-            nc.scalar.activation(out=sin_t[:, rows, :], in_=frac[:, rows, :], func=ACT.Sin, scale=2.0 * PI)
-            nc.scalar.activation(out=nsin_t[:, rows, :], in_=frac[:, rows, :], func=ACT.Sin, scale=-2.0 * PI)
             nc.scalar.activation(out=absf[:, rows, :], in_=frac[:, rows, :], func=ACT.Abs)
-            nc.scalar.activation(out=tab[:, rows, 2, :], in_=absf[:, rows, :], func=ACT.Sin, scale=-2.0 * PI, bias=0.5 * PI)
-            nc.gpsimd.tensor_tensor(out=tab[:, rows, 1, :], in0=sin_t[:, rows, :], in1=tab[:, rows, 2, :], op=ALU.subtract)
-            nc.gpsimd.tensor_tensor(out=tab[:, rows, 0, :], in0=nsin_t[:, rows, :], in1=tab[:, rows, 2, :], op=ALU.subtract)
+            nc.scalar.activation(out=tab[:, rows, 2, :], in_=frac[:, rows, :], func=ACT.Sin, scale=2.0 * PI)
+            nc.scalar.activation(out=cos_t[:, rows, :], in_=absf[:, rows, :], func=ACT.Sin, scale=-2.0 * PI, bias=0.5 * PI)
+            nc.gpsimd.tensor_tensor(out=tab[:, rows, 0, :], in0=cos_t[:, rows, :], in1=tab[:, rows, 2, :], op=ALU.subtract)
+            nc.gpsimd.tensor_tensor(out=tab[:, rows, 1, :], in0=cos_t[:, rows, :], in1=tab[:, rows, 2, :], op=ALU.add)
 
-        ctx.enter_context(tc.manual_schedule(engines={mybir.EngineType.DVE, mybir.EngineType.Activation}))
+        ctx.enter_context(tc.manual_schedule(engines={mybir.EngineType.DVE, mybir.EngineType.Activation, mybir.EngineType.PE}))
+        zeros = const.tile([P, 512], BF16, name="zeros")
+        nc.vector.memset(zeros[:], 0.0)
+        idle = ps_r.tile([P, 512], F32, name="idle", tag="mm")
+        for r in range(4):
+            nc.tensor.matmul(idle[:], lhsT=zeros[:, 0:P], rhs=zeros[:], start=True, stop=True)
         pos = const.tile([P, NI], F32, name="pos")
         nc.vector.tensor_copy(out=pos[:], in_=idx_i[:])
         turns = const.tile([P, HALF], F32, name="turns")
@@ -220,13 +224,13 @@ def tile_ropemaskedattentionhead_pa_t_kernel(tc, x_bytes, x_scale, w_q, w_k, w_v
         nc.vector.tensor_scalar(out=whole[:], in0=ang[:], scalar1=MAGIC, scalar2=MAGIC, op0=ALU.add, op1=ALU.subtract)
         frac = const.tile([P, NI, HALF], F32, name="frac")
         nc.vector.tensor_tensor(out=frac[:], in0=ang[:], in1=whole[:], op=ALU.subtract)
-        sin_t = const.tile([P, NI, HALF], F32, name="sin_t")
-        nsin_t = const.tile([P, NI, HALF], F32, name="nsin_t")
+        cos_t = const.tile([P, NI, HALF], F32, name="cos_t")
         absf = const.tile([P, NI, HALF], F32, name="absf")
         tab = const.tile([P, NI, 3, HALF], F32, name="tab")
 
-        wc = const.tile([P, 384], U32, name="wc", align_bytes=64)
-        ws = const.tile([P, 384], U8, name="ws", align_bytes=64)
+        wc = const.tile([P, 512], U32, name="wc", align_bytes=64)
+        ws = const.tile([P, 512], U8, name="ws", align_bytes=64)
+        wg_n = const.tile([P, 512], BF16, name="wg_n", align_bytes=64)
         wg_ab = const.tile([P, 1024], BF16, name="wg_ab", align_bytes=64)
         wg_c = const.tile([P, 512], BF16, name="wg_c", align_bytes=64)
         cast(0, 2)
@@ -240,8 +244,9 @@ def tile_ropemaskedattentionhead_pa_t_kernel(tc, x_bytes, x_scale, w_q, w_k, w_v
         for u in range(2):
             nc.tensor.transpose(tw2[:, u * P:(u + 1) * P], w_c[:].bitcast(F32)[:, u:256:2], ident[:])
         cast(1, 2)
-        for c in range(NI // GT):
-            table(c)
+        table(0)
+        cast(2, 1)
+        table(1)
 
         for m in range(-6, NM):
             if m >= 0 and m % 2 == 0:
@@ -254,6 +259,10 @@ def tile_ropemaskedattentionhead_pa_t_kernel(tc, x_bytes, x_scale, w_q, w_k, w_v
                 elif m + 1 == NM:
                     add_up(m - 1, nc.vector)
                     add_up(m, nc.vector)
+            if m == -2:
+                nc.vector.quantize_mx(out=wc[:, 0:256].bitcast(FP8X4), scales=ws[:, 0:256], in_=wg_ab[:])
+                nc.vector.quantize_mx(out=wc[:, 256:384].bitcast(FP8X4), scales=ws[:, 256:384], in_=wg_c[:])
+                nc.vector.quantize_mx(out=wc[:, 384:512].bitcast(FP8X4), scales=ws[:, 384:512], in_=wg_n[:])
             if 0 <= m + 3 < NM:
                 quant(m + 3)
             if 0 <= m + 2 < NM:
@@ -262,7 +271,9 @@ def tile_ropemaskedattentionhead_pa_t_kernel(tc, x_bytes, x_scale, w_q, w_k, w_v
                     mult_v((m + 2) // 2)
             if m + 6 in PLANE:
                 weave(m + 6)
-            if m % 2 == 0 and 2 <= m // 2 + 5 < NG:
+            if m in (-6, -4):
+                table(m // 2 + 5)
+            if m % 2 == 0 and 3 <= m // 2 + 5 < NG:
                 cast(m // 2 + 5, 1)
             if m + 8 in PLANE:
                 turn_y(m + 8)
@@ -273,11 +284,9 @@ def tile_ropemaskedattentionhead_pa_t_kernel(tc, x_bytes, x_scale, w_q, w_k, w_v
                     turn(WORD[k])
             elif m + 4 in PLANE and m + 5 < NM:
                 scale_out(m + 5, 0, P)
-            if m + 4 == 0:
+            if m + 4 == 1:
                 nc.vector.tensor_copy(out=wg_ab[:].bitcast(F32).rearrange("p (r u) -> p r u", u=2),
                                       in_=tw[:].rearrange("p (u r) -> p r u", u=2))
                 nc.vector.tensor_copy(out=wg_c[:].bitcast(F32).rearrange("p (r u) -> p r u", u=2),
                                       in_=tw2[:, 0:256].rearrange("p (u r) -> p r u", u=2))
-            if m + 4 == 1:
-                nc.vector.quantize_mx(out=wc[:, 0:256].bitcast(FP8X4), scales=ws[:, 0:256], in_=wg_ab[:])
-                nc.vector.quantize_mx(out=wc[:, 256:384].bitcast(FP8X4), scales=ws[:, 256:384], in_=wg_c[:])
+                nc.vector.tensor_scalar(out=wg_n[:], in0=wg_ab[:, 512:1024], scalar1=-1.0, scalar2=None, op0=ALU.mult)

@@ -45,33 +45,35 @@ def tile_ropemaskedattentionhead_pa_t_kernel(tc, x_bytes, x_scale, w_q, w_k, w_v
         xb = const.tile([P, NG * GT * D], U8, name="xb")
         XW = GT * D
 
-        def load(n, pieces):
+        def load(n, cuts):
             b, g = divmod(n, NI // GT)
-            step = XW // pieces
-            for c in range(pieces):
-                nc.sync.dma_start(out=xb[:, n * XW + c * step:n * XW + (c + 1) * step],
-                                  in_=x_views[b][:, g * XW + c * step:g * XW + (c + 1) * step])
+            for c0, c1 in zip(cuts[:-1], cuts[1:]):
+                nc.sync.dma_start(out=xb[:, n * XW + c0:n * XW + c1], in_=x_views[b][:, g * XW + c0:g * XW + c1])
 
-        load(0, 2)
+        FIRST = (0, D, 2 * D, XW)
+        WHOLE = (0, XW)
+        load(0, FIRST)
         w_a = const.tile([P, D], BF16, name="w_a")
         w_b = const.tile([P, D], BF16, name="w_b")
         w_c = const.tile([P, D], BF16, name="w_c")
         sc4 = const.tile([P, 4], F32, name="sc4")
         with nc.allow_non_contiguous_dma(reason="four scales to a partition"):
             nc.sync.dma_start(out=sc4[:], in_=x_scale.rearrange("a b (p t) -> p (a b t)", t=4))
-        load(1, 1)
+        load(1, WHOLE)
         nc.sync.dma_start(out=w_a[0:HALF, :], in_=w_q[0:HALF, :])
         nc.sync.dma_start(out=w_a[HALF:P, :], in_=w_k[0:HALF, :])
         nc.sync.dma_start(out=w_b[0:HALF, :], in_=w_q[HALF:HD, :])
         nc.sync.dma_start(out=w_b[HALF:P, :], in_=w_k[HALF:HD, :])
         nc.sync.dma_start(out=w_c[:], in_=w_v[:, :])
         for n in range(2, NG):
-            load(n, 1)
+            load(n, WHOLE)
 
-        idx_i = const.tile([P, NI], I32, name="idx_i")
-        nc.gpsimd.iota(idx_i[:], pattern=[[1, NI]], base=0, channel_multiplier=NI)
+        zeros = const.tile([P, 512], BF16, name="zeros")
+        nc.gpsimd.memset(zeros[:], 0.0)
         ident = const.tile([P, P], F32, name="ident")
         make_identity(nc, ident[:])
+        pos = const.tile([P, NI], F32, name="pos")
+        nc.gpsimd.iota(pos[:], pattern=[[1, NI]], base=0, channel_multiplier=NI, allow_small_or_imprecise_dtypes=True)
         ident_b = const.tile([P, P], BF16, name="ident_b")
         make_identity(nc, ident_b[:])
         one = const.tile([P, 1], F32, name="one")
@@ -81,12 +83,10 @@ def tile_ropemaskedattentionhead_pa_t_kernel(tc, x_bytes, x_scale, w_q, w_k, w_v
 
         st = {}
 
-        def cast(n, pieces):
+        def cast(n, cuts):
             xbf = work.tile([P, XW], BF16, name="xbf", tag="xbf", bufs=6)
-            step = XW // pieces
-            for c in range(pieces):
-                nc.scalar.copy(out=xbf[:, c * step:(c + 1) * step],
-                               in_=xb[:, n * XW + c * step:n * XW + (c + 1) * step].bitcast(FP8))
+            for c0, c1 in zip(cuts[:-1], cuts[1:]):
+                nc.scalar.copy(out=xbf[:, c0:c1], in_=xb[:, n * XW + c0:n * XW + c1].bitcast(FP8))
             st[("xbf", n)] = xbf
 
         def turn(m):
@@ -98,6 +98,23 @@ def tile_ropemaskedattentionhead_pa_t_kernel(tc, x_bytes, x_scale, w_q, w_k, w_v
                     nc.tensor.transpose(tp[:, u * 256 + a2 * P:u * 256 + (a2 + 1) * P],
                                         words[:, 256 * a + u:256 * (a + 1):2], ident[:])
             st[("tp", m)] = tp
+
+        def turn_first():
+            words = st[("xbf", 0)][:].bitcast(F32)
+            for a in range(2):
+                tp = ps_r.tile([P, 512], F32, name="tp", tag="mm")
+                for u in range(2):
+                    nc.tensor.transpose(tp[:, u * P:(u + 1) * P], words[:, 256 * a + u:256 * (a + 1):2], ident[:])
+                st[("tp0", a)] = tp
+
+        def scale_first():
+            grp = new_grp(0)
+            for a in range(2):
+                nc.vector.tensor_tensor(
+                    out=grp[:, 4 * P * a:4 * P * (a + 1)].rearrange("p (r u e) -> p r u e", u=2, e=2),
+                    in0=st[("tp0", a)][:, 0:2 * P].bitcast(BF16).rearrange("p (u r e) -> p r u e", u=2, e=2),
+                    in1=sc4[:].rearrange("p (u e) -> p u e", u=2).unsqueeze(1).to_broadcast([P, P, 2, 2]),
+                    op=ALU.mult)
 
         def turn_y(m):
             xbf = st[("xbf", m // 2)]
@@ -205,16 +222,13 @@ def tile_ropemaskedattentionhead_pa_t_kernel(tc, x_bytes, x_scale, w_q, w_k, w_v
             nc.gpsimd.tensor_tensor(out=tab[:, rows, 1, :], in0=cos_t[:, rows, :], in1=tab[:, rows, 2, :], op=ALU.add)
 
         ctx.enter_context(tc.manual_schedule(engines={mybir.EngineType.DVE, mybir.EngineType.Activation, mybir.EngineType.PE}))
-        zeros = const.tile([P, 512], BF16, name="zeros")
-        nc.vector.memset(zeros[:], 0.0)
         idle = ps_r.tile([P, 512], F32, name="idle", tag="mm")
         for r in range(4):
             nc.tensor.matmul(idle[:], lhsT=zeros[:, 0:P], rhs=zeros[:], start=True, stop=True)
-        pos = const.tile([P, NI], F32, name="pos")
-        nc.vector.tensor_copy(out=pos[:], in_=idx_i[:])
         turns = const.tile([P, HALF], F32, name="turns")
-        nc.vector.tensor_scalar(out=turns[:, 0:1], in0=one[:], scalar1=0.5 / PI, scalar2=None, op0=ALU.mult)
-        for m in range(6):
+        for j in range(8):
+            nc.vector.tensor_scalar(out=turns[:, j:j + 1], in0=one[:], scalar1=0.5 / PI * RATIO ** j, scalar2=None, op0=ALU.mult)
+        for m in range(3, 6):
             w = 1 << m
             nc.vector.tensor_scalar(out=turns[:, w:2 * w], in0=turns[:, 0:w], scalar1=RATIO ** w, scalar2=None, op0=ALU.mult)
         ang = const.tile([P, NI, HALF], F32, name="ang")
@@ -223,7 +237,6 @@ def tile_ropemaskedattentionhead_pa_t_kernel(tc, x_bytes, x_scale, w_q, w_k, w_v
         whole = const.tile([P, NI, HALF], I32, name="whole")
         nc.vector.tensor_scalar(out=whole[:], in0=ang[:], scalar1=MAGIC, scalar2=MAGIC, op0=ALU.add, op1=ALU.subtract)
         frac = const.tile([P, NI, HALF], F32, name="frac")
-        nc.vector.tensor_tensor(out=frac[:], in0=ang[:], in1=whole[:], op=ALU.subtract)
         cos_t = const.tile([P, NI, HALF], F32, name="cos_t")
         absf = const.tile([P, NI, HALF], F32, name="absf")
         tab = const.tile([P, NI, 3, HALF], F32, name="tab")
@@ -233,8 +246,8 @@ def tile_ropemaskedattentionhead_pa_t_kernel(tc, x_bytes, x_scale, w_q, w_k, w_v
         wg_n = const.tile([P, 512], BF16, name="wg_n", align_bytes=64)
         wg_ab = const.tile([P, 1024], BF16, name="wg_ab", align_bytes=64)
         wg_c = const.tile([P, 512], BF16, name="wg_c", align_bytes=64)
-        cast(0, 2)
-        turn(WORD[0])
+        cast(0, FIRST)
+        turn_first()
         turn(WORD[1])
         tw = ps_r.tile([P, 512], F32, name="tw", tag="mm")
         for a2, w_t in enumerate((w_a, w_b)):
@@ -243,10 +256,8 @@ def tile_ropemaskedattentionhead_pa_t_kernel(tc, x_bytes, x_scale, w_q, w_k, w_v
         tw2 = ps_r.tile([P, 512], F32, name="tw2", tag="mm")
         for u in range(2):
             nc.tensor.transpose(tw2[:, u * P:(u + 1) * P], w_c[:].bitcast(F32)[:, u:256:2], ident[:])
-        cast(1, 2)
-        table(0)
-        cast(2, 1)
-        table(1)
+        cast(1, (0, 2 * D, XW))
+        cast(2, WHOLE)
 
         for m in range(-6, NM):
             if m >= 0 and m % 2 == 0:
@@ -271,22 +282,28 @@ def tile_ropemaskedattentionhead_pa_t_kernel(tc, x_bytes, x_scale, w_q, w_k, w_v
                     mult_v((m + 2) // 2)
             if m + 6 in PLANE:
                 weave(m + 6)
-            if m in (-6, -4):
-                table(m // 2 + 5)
             if m % 2 == 0 and 3 <= m // 2 + 5 < NG:
-                cast(m // 2 + 5, 1)
+                cast(m // 2 + 5, WHOLE)
             if m + 8 in PLANE:
                 turn_y(m + 8)
-            if m + 4 in WORD:
+            if m == -4:
+                scale_first()
+                turn(WORD[2])
+                nc.vector.tensor_tensor(out=frac[:], in0=ang[:], in1=whole[:], op=ALU.subtract)
+                table(0)
+                table(1)
+            elif m + 4 in WORD:
                 scale_out(m + 4, P if m + 3 in PLANE else 0, 2 * P)
                 k = WORD.index(m + 4) + 2
                 if k < len(WORD):
                     turn(WORD[k])
             elif m + 4 in PLANE and m + 5 < NM:
                 scale_out(m + 5, 0, P)
-            if m + 4 == 1:
+            if m == -3:
                 nc.vector.tensor_copy(out=wg_ab[:].bitcast(F32).rearrange("p (r u) -> p r u", u=2),
                                       in_=tw[:].rearrange("p (u r) -> p r u", u=2))
                 nc.vector.tensor_copy(out=wg_c[:].bitcast(F32).rearrange("p (r u) -> p r u", u=2),
                                       in_=tw2[:, 0:256].rearrange("p (u r) -> p r u", u=2))
                 nc.vector.tensor_scalar(out=wg_n[:], in0=wg_ab[:, 512:1024], scalar1=-1.0, scalar2=None, op0=ALU.mult)
+                table(2)
+                table(3)

@@ -25,7 +25,7 @@ NM = 2 * NG
 PI = 3.141592653589793
 RATIO = 10000.0 ** (-1.0 / HALF)
 MAGIC = 8388608.0
-PLANE = frozenset(2 * g + 1 for g in range(2, NG) if g not in (6, 10))
+PLANE = frozenset(2 * g + 1 for g in range(2, NG) if g not in (5, 9))
 WORD = tuple(m for m in range(NM) if m not in PLANE)
 
 
@@ -60,20 +60,20 @@ def tile_ropemaskedattentionhead_pa_t_kernel(tc, x_bytes, x_scale, w_q, w_k, w_v
         with nc.allow_non_contiguous_dma(reason="four scales to a partition"):
             nc.sync.dma_start(out=sc4[:], in_=x_scale.rearrange("a b (p t) -> p (a b t)", t=4))
         load(1, WHOLE)
-        nc.sync.dma_start(out=w_a[0:HALF, :], in_=w_q[0:HALF, :])
-        nc.sync.dma_start(out=w_a[HALF:P, :], in_=w_k[0:HALF, :])
-        nc.sync.dma_start(out=w_b[0:HALF, :], in_=w_q[HALF:HD, :])
-        nc.sync.dma_start(out=w_b[HALF:P, :], in_=w_k[HALF:HD, :])
+        nc.sync.dma_start(out=w_a[0:HALF, :], in_=w_q[HALF:HD, :])
+        nc.sync.dma_start(out=w_a[HALF:P, :], in_=w_k[HALF:HD, :])
+        nc.sync.dma_start(out=w_b[0:HALF, :], in_=w_q[0:HALF, :])
+        nc.sync.dma_start(out=w_b[HALF:P, :], in_=w_k[0:HALF, :])
         nc.sync.dma_start(out=w_c[:], in_=w_v[:, :])
         for n in range(2, NG):
             load(n, WHOLE)
 
+        pos = const.tile([P, NI], F32, name="pos")
+        nc.gpsimd.iota(pos[:], pattern=[[1, NI]], base=0, channel_multiplier=NI, allow_small_or_imprecise_dtypes=True)
         zeros = const.tile([P, 512], BF16, name="zeros")
         nc.gpsimd.memset(zeros[:], 0.0)
         ident = const.tile([P, P], F32, name="ident")
         make_identity(nc, ident[:])
-        pos = const.tile([P, NI], F32, name="pos")
-        nc.gpsimd.iota(pos[:], pattern=[[1, NI]], base=0, channel_multiplier=NI, allow_small_or_imprecise_dtypes=True)
         ident_b = const.tile([P, P], BF16, name="ident_b")
         make_identity(nc, ident_b[:])
         one = const.tile([P, 1], F32, name="one")
@@ -108,7 +108,7 @@ def tile_ropemaskedattentionhead_pa_t_kernel(tc, x_bytes, x_scale, w_q, w_k, w_v
                 st[("tp0", a)] = tp
 
         def scale_first():
-            grp = new_grp(0)
+            grp = pair_of_grp(0)
             for a in range(2):
                 nc.vector.tensor_tensor(
                     out=grp[:, 4 * P * a:4 * P * (a + 1)].rearrange("p (r u e) -> p r u e", u=2, e=2),
@@ -129,28 +129,30 @@ def tile_ropemaskedattentionhead_pa_t_kernel(tc, x_bytes, x_scale, w_q, w_k, w_v
                 nc.scalar.activation(out=pl[:, t, :], in_=tpb[:, t * 256:(t + 1) * 256], func=ACT.Copy, scale=sc4[:, t:t + 1])
             st[("pl", m)] = pl
 
-        def new_grp(m):
-            st[("grp", m)] = work.tile([P, 2 * P * 4], BF16, name="grp", tag="grp", align_bytes=64)
-            return st[("grp", m)]
+        def pair_of_grp(m):
+            n, h = divmod(m, 2)
+            if ("grp", n) not in st:
+                st[("grp", n)] = work.tile([P, GT * P * 4], BF16, name="grp", tag="grp", align_bytes=64)
+            return st[("grp", n)][:, h * 2 * P * 4:(h + 1) * 2 * P * 4]
 
         def weave(m):
-            nc.scalar.copy(out=new_grp(m)[:].rearrange("p (c i t) -> p c t i", i=4, t=4),
+            nc.scalar.copy(out=pair_of_grp(m).rearrange("p (c i t) -> p c t i", i=4, t=4),
                            in_=st[("pl", m)][:].rearrange("p t (c i) -> p c t i", i=4))
 
         def scale_out(m, r0, r1):
-            grp = new_grp(m) if r0 == 0 else st[("grp", m)]
             nc.vector.tensor_tensor(
-                out=grp[:, 4 * r0:4 * r1].rearrange("p (r u e) -> p r u e", u=2, e=2),
+                out=pair_of_grp(m)[:, 4 * r0:4 * r1].rearrange("p (r u e) -> p r u e", u=2, e=2),
                 in0=st[("tp", m)][:].bitcast(BF16).rearrange("p (u r e) -> p r u e", u=2, e=2)[:, r0:r1, :, :],
                 in1=sc4[:].rearrange("p (u e) -> p u e", u=2).unsqueeze(1).to_broadcast([P, r1 - r0, 2, 2]),
                 op=ALU.mult)
 
-        def quant(m):
-            codes = work.tile([P, 2 * P], U32, name="codes", tag="codes", align_bytes=64, bufs=6)
-            xs = work.tile([P, 2 * P], U8, name="xs", tag="xs", align_bytes=64, bufs=6)
-            nc.vector.quantize_mx(out=codes[:].bitcast(FP8X4), scales=xs[:], in_=st[("grp", m)][:])
-            st[("codes", m)] = codes
-            st[("xs", m)] = xs
+        def quant(n):
+            codes = work.tile([P, GT * P], U32, name="codes", tag="codes", align_bytes=64)
+            xs = work.tile([P, GT * P], U8, name="xs", tag="xs", align_bytes=64)
+            nc.vector.quantize_mx(out=codes[:].bitcast(FP8X4), scales=xs[:], in_=st[("grp", n)][:])
+            for h in range(2):
+                st[("codes", 2 * n + h)] = codes[:, h * 2 * P:(h + 1) * 2 * P]
+                st[("xs", 2 * n + h)] = xs[:, h * 2 * P:(h + 1) * 2 * P]
 
         def mult(m):
             codes, xs = st[("codes", m)], st[("xs", m)]
@@ -163,8 +165,8 @@ def tile_ropemaskedattentionhead_pa_t_kernel(tc, x_bytes, x_scale, w_q, w_k, w_v
                                     rhs_scale=ws[:, 0:256], start=True, stop=True)
                 nc.tensor.matmul_mx(out=mm[:, 256:384], lhsT=lt, lhsT_scale=ls, rhs=wc[:, 0:128].bitcast(FP8X4),
                                     rhs_scale=ws[:, 0:128], start=True, stop=False)
-                nc.tensor.matmul_mx(out=mm[:, 256:384], lhsT=lt, lhsT_scale=ls, rhs=wc[:, 384:512].bitcast(FP8X4),
-                                    rhs_scale=ws[:, 384:512], start=False, stop=True)
+                nc.tensor.matmul_mx(out=mm[:, 256:384], lhsT=lt, lhsT_scale=ls, rhs=wc[:, 128:256].bitcast(FP8X4),
+                                    rhs_scale=ws[:, 128:256], start=False, stop=True)
 
         def mult_v(n):
             vb = ps_v.tile([P, GT * HD], F32, name="vb", tag="vb")
@@ -197,7 +199,7 @@ def tile_ropemaskedattentionhead_pa_t_kernel(tc, x_bytes, x_scale, w_q, w_k, w_v
             eng.tensor_tensor(
                 out=o_r[:, :, a0 * HD:a1 * HD].rearrange("p w (a h j) -> p a w h j", h=2, j=HALF),
                 in0=prod[:, :, :, 0:2, :],
-                in1=prod[:, :, :, 2:3, :].to_broadcast([P, 2, 2, 2, HALF]), op=ALU.add)
+                in1=prod[:, :, :, 2:3, :].to_broadcast([P, 2, 2, 2, HALF]), op=ALU.subtract)
             if n + 1 == NG:
                 s0, s1 = a0, a1
             elif h == 1:
@@ -216,34 +218,44 @@ def tile_ropemaskedattentionhead_pa_t_kernel(tc, x_bytes, x_scale, w_q, w_k, w_v
         def table(c):
             rows = slice(c * GT, (c + 1) * GT)
             nc.scalar.activation(out=absf[:, rows, :], in_=frac[:, rows, :], func=ACT.Abs)
-            nc.scalar.activation(out=tab[:, rows, 2, :], in_=frac[:, rows, :], func=ACT.Sin, scale=2.0 * PI)
-            nc.scalar.activation(out=cos_t[:, rows, :], in_=absf[:, rows, :], func=ACT.Sin, scale=-2.0 * PI, bias=0.5 * PI)
-            nc.gpsimd.tensor_tensor(out=tab[:, rows, 0, :], in0=cos_t[:, rows, :], in1=tab[:, rows, 2, :], op=ALU.subtract)
-            nc.gpsimd.tensor_tensor(out=tab[:, rows, 1, :], in0=cos_t[:, rows, :], in1=tab[:, rows, 2, :], op=ALU.add)
+            nc.scalar.activation(out=sin_t[:, rows, :], in_=frac[:, rows, :], func=ACT.Sin, scale=2.0 * PI)
+            nc.scalar.activation(out=tab[:, rows, 2, :], in_=absf[:, rows, :], func=ACT.Sin, scale=2.0 * PI, bias=-0.5 * PI)
+            nc.gpsimd.tensor_tensor(out=tab[:, rows, 0, :], in0=tab[:, rows, 2, :], in1=sin_t[:, rows, :], op=ALU.subtract)
+            nc.gpsimd.tensor_tensor(out=tab[:, rows, 1, :], in0=tab[:, rows, 2, :], in1=sin_t[:, rows, :], op=ALU.add)
 
         ctx.enter_context(tc.manual_schedule(engines={mybir.EngineType.DVE, mybir.EngineType.Activation, mybir.EngineType.PE}))
         idle = ps_r.tile([P, 512], F32, name="idle", tag="mm")
         for r in range(4):
             nc.tensor.matmul(idle[:], lhsT=zeros[:, 0:P], rhs=zeros[:], start=True, stop=True)
         turns = const.tile([P, HALF], F32, name="turns")
+        fine = const.tile([P, 8], F32, name="fine")
+        coarse = const.tile([P, 8], F32, name="coarse")
         for j in range(8):
-            nc.vector.tensor_scalar(out=turns[:, j:j + 1], in0=one[:], scalar1=0.5 / PI * RATIO ** j, scalar2=None, op0=ALU.mult)
-        for m in range(3, 6):
-            w = 1 << m
-            nc.vector.tensor_scalar(out=turns[:, w:2 * w], in0=turns[:, 0:w], scalar1=RATIO ** w, scalar2=None, op0=ALU.mult)
+            nc.vector.tensor_scalar(out=fine[:, j:j + 1], in0=one[:], scalar1=0.5 / PI * RATIO ** j, scalar2=None, op0=ALU.mult)
+            nc.vector.tensor_scalar(out=coarse[:, j:j + 1], in0=one[:], scalar1=RATIO ** (8 * j), scalar2=None, op0=ALU.mult)
+        nc.vector.tensor_tensor(out=turns[:].rearrange("p (u v) -> p u v", v=8), in0=coarse[:].unsqueeze(2).to_broadcast([P, 8, 8]),
+                                in1=fine[:].unsqueeze(1).to_broadcast([P, 8, 8]), op=ALU.mult)
         ang = const.tile([P, NI, HALF], F32, name="ang")
-        nc.vector.tensor_tensor(out=ang[:], in0=pos[:].unsqueeze(2).to_broadcast([P, NI, HALF]),
-                                in1=turns[:].unsqueeze(1).to_broadcast([P, NI, HALF]), op=ALU.mult)
         whole = const.tile([P, NI, HALF], I32, name="whole")
-        nc.vector.tensor_scalar(out=whole[:], in0=ang[:], scalar1=MAGIC, scalar2=MAGIC, op0=ALU.add, op1=ALU.subtract)
         frac = const.tile([P, NI, HALF], F32, name="frac")
-        cos_t = const.tile([P, NI, HALF], F32, name="cos_t")
+        chunks = [slice(c * GT, (c + 1) * GT) for c in range(NI // GT)]
+        for c in range(len(chunks) + 2):
+            if c < len(chunks):
+                r = chunks[c]
+                nc.vector.tensor_tensor(out=ang[:, r, :], in0=pos[:, r].unsqueeze(2).to_broadcast([P, GT, HALF]),
+                                        in1=turns[:].unsqueeze(1).to_broadcast([P, GT, HALF]), op=ALU.mult)
+            if 0 <= c - 1 < len(chunks):
+                r = chunks[c - 1]
+                nc.vector.tensor_scalar(out=whole[:, r, :], in0=ang[:, r, :], scalar1=MAGIC, scalar2=MAGIC, op0=ALU.add, op1=ALU.subtract)
+            if 0 <= c - 2:
+                r = chunks[c - 2]
+                nc.vector.tensor_tensor(out=frac[:, r, :], in0=ang[:, r, :], in1=whole[:, r, :], op=ALU.subtract)
+        sin_t = const.tile([P, NI, HALF], F32, name="sin_t")
         absf = const.tile([P, NI, HALF], F32, name="absf")
         tab = const.tile([P, NI, 3, HALF], F32, name="tab")
 
-        wc = const.tile([P, 512], U32, name="wc", align_bytes=64)
-        ws = const.tile([P, 512], U8, name="ws", align_bytes=64)
-        wg_n = const.tile([P, 512], BF16, name="wg_n", align_bytes=64)
+        wc = const.tile([P, 384], U32, name="wc", align_bytes=64)
+        ws = const.tile([P, 384], U8, name="ws", align_bytes=64)
         wg_ab = const.tile([P, 1024], BF16, name="wg_ab", align_bytes=64)
         wg_c = const.tile([P, 512], BF16, name="wg_c", align_bytes=64)
         cast(0, FIRST)
@@ -257,7 +269,10 @@ def tile_ropemaskedattentionhead_pa_t_kernel(tc, x_bytes, x_scale, w_q, w_k, w_v
         for u in range(2):
             nc.tensor.transpose(tw2[:, u * P:(u + 1) * P], w_c[:].bitcast(F32)[:, u:256:2], ident[:])
         cast(1, (0, 2 * D, XW))
+        table(0)
         cast(2, WHOLE)
+        for c in range(1, NI // GT):
+            table(c)
 
         for m in range(-6, NM):
             if m >= 0 and m % 2 == 0:
@@ -273,9 +288,8 @@ def tile_ropemaskedattentionhead_pa_t_kernel(tc, x_bytes, x_scale, w_q, w_k, w_v
             if m == -2:
                 nc.vector.quantize_mx(out=wc[:, 0:256].bitcast(FP8X4), scales=ws[:, 0:256], in_=wg_ab[:])
                 nc.vector.quantize_mx(out=wc[:, 256:384].bitcast(FP8X4), scales=ws[:, 256:384], in_=wg_c[:])
-                nc.vector.quantize_mx(out=wc[:, 384:512].bitcast(FP8X4), scales=ws[:, 384:512], in_=wg_n[:])
-            if 0 <= m + 3 < NM:
-                quant(m + 3)
+            if m % 2 == 0 and 0 <= m + 2 < NM:
+                quant((m + 2) // 2)
             if 0 <= m + 2 < NM:
                 mult(m + 2)
                 if m % 2 == 1:
@@ -289,9 +303,6 @@ def tile_ropemaskedattentionhead_pa_t_kernel(tc, x_bytes, x_scale, w_q, w_k, w_v
             if m == -4:
                 scale_first()
                 turn(WORD[2])
-                nc.vector.tensor_tensor(out=frac[:], in0=ang[:], in1=whole[:], op=ALU.subtract)
-                table(0)
-                table(1)
             elif m + 4 in WORD:
                 scale_out(m + 4, P if m + 3 in PLANE else 0, 2 * P)
                 k = WORD.index(m + 4) + 2
@@ -304,6 +315,3 @@ def tile_ropemaskedattentionhead_pa_t_kernel(tc, x_bytes, x_scale, w_q, w_k, w_v
                                       in_=tw[:].rearrange("p (u r) -> p r u", u=2))
                 nc.vector.tensor_copy(out=wg_c[:].bitcast(F32).rearrange("p (r u) -> p r u", u=2),
                                       in_=tw2[:, 0:256].rearrange("p (u r) -> p r u", u=2))
-                nc.vector.tensor_scalar(out=wg_n[:], in0=wg_ab[:, 512:1024], scalar1=-1.0, scalar2=None, op0=ALU.mult)
-                table(2)
-                table(3)

@@ -26,6 +26,7 @@ PI = 3.141592653589793
 RATIO = 10000.0 ** (-1.0 / HALF)
 MAGIC = 8388608.0
 PLANE = frozenset(2 * g + 1 for g in range(2, NG) if g not in (5, 9))
+BY_PRODUCT = frozenset(m for m in PLANE if m < 24)
 WORD = tuple(m for m in range(NM) if m not in PLANE)
 
 
@@ -122,8 +123,12 @@ def tile_ropemaskedattentionhead_pa_t_kernel(tc, x_bytes, x_scale, w_q, w_k, w_v
             for a2 in range(2):
                 a = 2 * (m % 2) + a2
                 for t in range(4):
-                    nc.tensor.transpose(tpb[:, t * 256 + a2 * P:t * 256 + (a2 + 1) * P],
-                                        xbf[:, a * D + t:(a + 1) * D:4], ident_b[:])
+                    block = tpb[:, t * 256 + a2 * P:t * 256 + (a2 + 1) * P]
+                    plane = xbf[:, a * D + t:(a + 1) * D:4]
+                    if m in BY_PRODUCT:
+                        nc.tensor.matmul(block, lhsT=plane, rhs=ident_b[:], start=True, stop=True)
+                    else:
+                        nc.tensor.transpose(block, plane, ident_b[:])
             pl = work.tile([P, 4, 256], BF16, name="pl", tag="pl")
             for t in range(4):
                 nc.scalar.activation(out=pl[:, t, :], in_=tpb[:, t * 256:(t + 1) * 256], func=ACT.Copy, scale=sc4[:, t:t + 1])
@@ -225,7 +230,7 @@ def tile_ropemaskedattentionhead_pa_t_kernel(tc, x_bytes, x_scale, w_q, w_k, w_v
 
         ctx.enter_context(tc.manual_schedule(engines={mybir.EngineType.DVE, mybir.EngineType.Activation, mybir.EngineType.PE}))
         idle = ps_r.tile([P, 512], F32, name="idle", tag="mm")
-        for r in range(4):
+        for r in range(3):
             nc.tensor.matmul(idle[:], lhsT=zeros[:, 0:P], rhs=zeros[:], start=True, stop=True)
         turns = const.tile([P, HALF], F32, name="turns")
         fine = const.tile([P, 8], F32, name="fine")

from contextlib import ExitStack

import concourse.mybir as mybir
from concourse.masks import make_identity

B, S, D, HD = 4, 2048, 512, 128
HALF = HD // 2
FLOPS = 2 * B * S * D * 3 * HD

F32 = mybir.dt.float32
BF16 = mybir.dt.bfloat16
I32 = mybir.dt.int32
U32 = mybir.dt.uint32
U8 = mybir.dt.uint8
FP8 = mybir.dt.float8_e4m3fn
FP8X4 = mybir.dt.float8_e4m3fn_x4
ALU = mybir.AluOpType
ACT = mybir.ActivationFunctionType

P = 128
NI = S // P
GT = 4
NG = B * NI // GT
NM = 2 * NG
PI = 3.141592653589793
RATIO = 10000.0 ** (-1.0 / HALF)
MAGIC = 8388608.0
PLANE = frozenset(2 * g + 1 for g in range(2, NG) if g not in (5, 9))
BY_PRODUCT = frozenset(m for m in PLANE if m < 24)
WORD = tuple(m for m in range(NM) if m not in PLANE)


def tile_ropemaskedattentionhead_pa_t_kernel(tc, x_bytes, x_scale, w_q, w_k, w_v, out_0, out_1, out_2):
    nc = tc.nc
    with ExitStack() as ctx:
        const = ctx.enter_context(tc.tile_pool(name="const", bufs=1))
        work = ctx.enter_context(tc.tile_pool(name="work", bufs=4))
        ps_t = ctx.enter_context(tc.psum_pool(name="ps_t", bufs=2))
        ps_y = ctx.enter_context(tc.psum_pool(name="ps_y", bufs=1))
        ps_r = ctx.enter_context(tc.psum_pool(name="ps_r", bufs=4))
        ps_v = ctx.enter_context(tc.psum_pool(name="ps_v", bufs=1))

        x_views = [x_bytes[b].rearrange("(p i) k -> p (i k)", i=NI) for b in range(B)]
        o_views = [[o[b].rearrange("(p i) d -> p (i d)", i=NI) for b in range(B)] for o in (out_0, out_1, out_2)]

        xb = const.tile([P, NG * GT * D], U8, name="xb")
        XW = GT * D

        def load(n, cuts):
            b, g = divmod(n, NI // GT)
            for c0, c1 in zip(cuts[:-1], cuts[1:]):
                nc.sync.dma_start(out=xb[:, n * XW + c0:n * XW + c1], in_=x_views[b][:, g * XW + c0:g * XW + c1])

        FIRST = (0, D, 2 * D, XW)
        WHOLE = (0, XW)
        load(0, FIRST)
        w_a = const.tile([P, D], BF16, name="w_a")
        w_b = const.tile([P, D], BF16, name="w_b")
        w_c = const.tile([P, D], BF16, name="w_c")
        sc4 = const.tile([P, 4], F32, name="sc4")
        with nc.allow_non_contiguous_dma(reason="four scales to a partition"):
            nc.sync.dma_start(out=sc4[:], in_=x_scale.rearrange("a b (p t) -> p (a b t)", t=4))
        load(1, WHOLE)
        nc.sync.dma_start(out=w_a[0:HALF, :], in_=w_q[HALF:HD, :])
        nc.sync.dma_start(out=w_a[HALF:P, :], in_=w_k[HALF:HD, :])
        nc.sync.dma_start(out=w_b[0:HALF, :], in_=w_q[0:HALF, :])
        nc.sync.dma_start(out=w_b[HALF:P, :], in_=w_k[0:HALF, :])
        nc.sync.dma_start(out=w_c[:], in_=w_v[:, :])
        for n in range(2, NG):
            load(n, WHOLE)

        pos = const.tile([P, NI], F32, name="pos")
        nc.gpsimd.iota(pos[:], pattern=[[1, NI]], base=0, channel_multiplier=NI, allow_small_or_imprecise_dtypes=True)
        zeros = const.tile([P, 512], BF16, name="zeros")
        nc.gpsimd.memset(zeros[:], 0.0)
        ident = const.tile([P, P], F32, name="ident")
        make_identity(nc, ident[:])
        ident_b = const.tile([P, P], BF16, name="ident_b")
        make_identity(nc, ident_b[:])
        one = const.tile([P, 1], F32, name="one")
        nc.vector.memset(one[:], 1.0)
        junk = const.tile([P, 1], F32, name="junk")
        nc.scalar.activation(out=junk[:], in_=one[:], func=ACT.Sin)

        st = {}

        def cast(n, cuts):
            xbf = work.tile([P, XW], BF16, name="xbf", tag="xbf", bufs=6)
            for c0, c1 in zip(cuts[:-1], cuts[1:]):
                nc.scalar.copy(out=xbf[:, c0:c1], in_=xb[:, n * XW + c0:n * XW + c1].bitcast(FP8))
            st[("xbf", n)] = xbf

        def turn(m):
            words = st[("xbf", m // 2)][:].bitcast(F32)
            tp = ps_t.tile([P, 512], F32, name="tp", tag="tp")
            for a2 in range(2):
                a = 2 * (m % 2) + a2
                for u in range(2):
                    nc.tensor.transpose(tp[:, u * 256 + a2 * P:u * 256 + (a2 + 1) * P],
                                        words[:, 256 * a + u:256 * (a + 1):2], ident[:])
            st[("tp", m)] = tp

        def turn_first():
            words = st[("xbf", 0)][:].bitcast(F32)
            for a in range(2):
                tp = ps_r.tile([P, 512], F32, name="tp", tag="mm")
                for u in range(2):
                    nc.tensor.transpose(tp[:, u * P:(u + 1) * P], words[:, 256 * a + u:256 * (a + 1):2], ident[:])
                st[("tp0", a)] = tp

        def scale_first():
            grp = pair_of_grp(0)
            for a in range(2):
                nc.vector.tensor_tensor(
                    out=grp[:, 4 * P * a:4 * P * (a + 1)].rearrange("p (r u e) -> p r u e", u=2, e=2),
                    in0=st[("tp0", a)][:, 0:2 * P].bitcast(BF16).rearrange("p (u r e) -> p r u e", u=2, e=2),
                    in1=sc4[:].rearrange("p (u e) -> p u e", u=2).unsqueeze(1).to_broadcast([P, P, 2, 2]),
                    op=ALU.mult)

        def turn_y(m):
            xbf = st[("xbf", m // 2)]
            tpb = ps_y.tile([P, 1024], BF16, name="tpb", tag="tpb")
            for a2 in range(2):
                a = 2 * (m % 2) + a2
                for t in range(4):
                    block = tpb[:, t * 256 + a2 * P:t * 256 + (a2 + 1) * P]
                    plane = xbf[:, a * D + t:(a + 1) * D:4]
                    if m in BY_PRODUCT:
                        nc.tensor.matmul(block, lhsT=plane, rhs=ident_b[:], start=True, stop=True)
                    else:
                        nc.tensor.transpose(block, plane, ident_b[:])
            pl = work.tile([P, 4, 256], BF16, name="pl", tag="pl")
            for t in range(4):
                nc.scalar.activation(out=pl[:, t, :], in_=tpb[:, t * 256:(t + 1) * 256], func=ACT.Copy, scale=sc4[:, t:t + 1])
            st[("pl", m)] = pl

        def pair_of_grp(m):
            n, h = divmod(m, 2)
            if ("grp", n) not in st:
                st[("grp", n)] = work.tile([P, GT * P * 4], BF16, name="grp", tag="grp", align_bytes=64)
            return st[("grp", n)][:, h * 2 * P * 4:(h + 1) * 2 * P * 4]

        def weave(m):
            nc.scalar.copy(out=pair_of_grp(m).rearrange("p (c i t) -> p c t i", i=4, t=4),
                           in_=st[("pl", m)][:].rearrange("p t (c i) -> p c t i", i=4))

        def scale_out(m, r0, r1):
            nc.vector.tensor_tensor(
                out=pair_of_grp(m)[:, 4 * r0:4 * r1].rearrange("p (r u e) -> p r u e", u=2, e=2),
                in0=st[("tp", m)][:].bitcast(BF16).rearrange("p (u r e) -> p r u e", u=2, e=2)[:, r0:r1, :, :],
                in1=sc4[:].rearrange("p (u e) -> p u e", u=2).unsqueeze(1).to_broadcast([P, r1 - r0, 2, 2]),
                op=ALU.mult)

        def quant(n):
            codes = work.tile([P, GT * P], U32, name="codes", tag="codes", align_bytes=64)
            xs = work.tile([P, GT * P], U8, name="xs", tag="xs", align_bytes=64)
            nc.vector.quantize_mx(out=codes[:].bitcast(FP8X4), scales=xs[:], in_=st[("grp", n)][:])
            for h in range(2):
                st[("codes", 2 * n + h)] = codes[:, h * 2 * P:(h + 1) * 2 * P]
                st[("xs", 2 * n + h)] = xs[:, h * 2 * P:(h + 1) * 2 * P]

        def mult(m):
            codes, xs = st[("codes", m)], st[("xs", m)]
            for a2 in range(2):
                mm = ps_r.tile([P, 512], F32, name="mm", tag="mm")
                st[("mm", m, a2)] = mm
                lt = codes[:, a2 * P:(a2 + 1) * P].bitcast(FP8X4)
                ls = xs[:, a2 * P:(a2 + 1) * P]
                nc.tensor.matmul_mx(out=mm[:, 0:256], lhsT=lt, lhsT_scale=ls, rhs=wc[:, 0:256].bitcast(FP8X4),
                                    rhs_scale=ws[:, 0:256], start=True, stop=True)
                nc.tensor.matmul_mx(out=mm[:, 256:384], lhsT=lt, lhsT_scale=ls, rhs=wc[:, 0:128].bitcast(FP8X4),
                                    rhs_scale=ws[:, 0:128], start=True, stop=False)
                nc.tensor.matmul_mx(out=mm[:, 256:384], lhsT=lt, lhsT_scale=ls, rhs=wc[:, 128:256].bitcast(FP8X4),
                                    rhs_scale=ws[:, 128:256], start=False, stop=True)

        def mult_v(n):
            vb = ps_v.tile([P, GT * HD], F32, name="vb", tag="vb")
            for a in range(GT):
                m, a2 = 2 * n + a // 2, a % 2
                nc.tensor.matmul_mx(out=vb[:, a * HD:(a + 1) * HD],
                                    lhsT=st[("codes", m)][:, a2 * P:(a2 + 1) * P].bitcast(FP8X4),
                                    lhsT_scale=st[("xs", m)][:, a2 * P:(a2 + 1) * P],
                                    rhs=wc[:, 256:384].bitcast(FP8X4), rhs_scale=ws[:, 256:384], start=True, stop=True)
            st[("vb", n)] = vb

        def rope(m, a2):
            if a2 == 0:
                st[("prod", m)] = work.tile([P, 2, 2, 3, HALF], F32, name="prod", tag="prod")
            prod = st[("prod", m)]
            i = ((m // 2) % (NI // GT)) * GT + 2 * (m % 2) + a2
            nc.vector.tensor_tensor(
                out=prod[:, a2, :, :, :].rearrange("p w c j -> p c w j"),
                in0=st[("mm", m, a2)][:, 0:384].rearrange("p (c w j) -> p c w j", c=3, w=2),
                in1=tab[:, i, :, :].unsqueeze(2).to_broadcast([P, 3, 2, HALF]),
                op=ALU.mult)

        def add_up(m, eng):
            n, h = divmod(m, 2)
            if h == 0:
                st[("o_r", n)] = work.tile([P, 2, GT * HD], F32, name="o_r", tag="o_r")
            b, g = divmod(n, NI // GT)
            o_r, prod = st[("o_r", n)], st[("prod", m)]
            a0, a1 = 2 * h, 2 * h + 2
            eng.tensor_tensor(
                out=o_r[:, :, a0 * HD:a1 * HD].rearrange("p w (a h j) -> p a w h j", h=2, j=HALF),
                in0=prod[:, :, :, 0:2, :],
                in1=prod[:, :, :, 2:3, :].to_broadcast([P, 2, 2, 2, HALF]), op=ALU.subtract)
            if n + 1 == NG:
                s0, s1 = a0, a1
            elif h == 1:
                s0, s1 = 0, GT
            else:
                return
            for w in range(2):
                nc.sync.dma_start(out=o_views[w][b][:, (g * GT + s0) * HD:(g * GT + s1) * HD], in_=o_r[:, w, s0 * HD:s1 * HD])

        def finish_v(n):
            b, g = divmod(n, NI // GT)
            o_v = work.tile([P, GT * HD], F32, name="o_v", tag="o_v")
            nc.scalar.copy(out=o_v[:], in_=st[("vb", n)][:])
            nc.sync.dma_start(out=o_views[2][b][:, g * GT * HD:(g + 1) * GT * HD], in_=o_v[:])

        def table(c):
            rows = slice(c * GT, (c + 1) * GT)
            nc.scalar.activation(out=absf[:, rows, :], in_=frac[:, rows, :], func=ACT.Abs)
            nc.scalar.activation(out=sin_t[:, rows, :], in_=frac[:, rows, :], func=ACT.Sin, scale=2.0 * PI)
            nc.scalar.activation(out=tab[:, rows, 2, :], in_=absf[:, rows, :], func=ACT.Sin, scale=2.0 * PI, bias=-0.5 * PI)
            nc.gpsimd.tensor_tensor(out=tab[:, rows, 0, :], in0=tab[:, rows, 2, :], in1=sin_t[:, rows, :], op=ALU.subtract)
            nc.gpsimd.tensor_tensor(out=tab[:, rows, 1, :], in0=tab[:, rows, 2, :], in1=sin_t[:, rows, :], op=ALU.add)

        ctx.enter_context(tc.manual_schedule(engines={mybir.EngineType.DVE, mybir.EngineType.Activation, mybir.EngineType.PE}))
        idle = ps_r.tile([P, 512], F32, name="idle", tag="mm")
        for r in range(3):
            nc.tensor.matmul(idle[:], lhsT=zeros[:, 0:P], rhs=zeros[:], start=True, stop=True)
        turns = const.tile([P, HALF], F32, name="turns")
        fine = const.tile([P, 8], F32, name="fine")
        coarse = const.tile([P, 8], F32, name="coarse")
        for j in range(8):
            nc.vector.tensor_scalar(out=fine[:, j:j + 1], in0=one[:], scalar1=0.5 / PI * RATIO ** j, scalar2=None, op0=ALU.mult)
            nc.vector.tensor_scalar(out=coarse[:, j:j + 1], in0=one[:], scalar1=RATIO ** (8 * j), scalar2=None, op0=ALU.mult)
        nc.vector.tensor_tensor(out=turns[:].rearrange("p (u v) -> p u v", v=8), in0=coarse[:].unsqueeze(2).to_broadcast([P, 8, 8]),
                                in1=fine[:].unsqueeze(1).to_broadcast([P, 8, 8]), op=ALU.mult)
        ang = const.tile([P, NI, HALF], F32, name="ang")
        whole = const.tile([P, NI, HALF], I32, name="whole")
        frac = const.tile([P, NI, HALF], F32, name="frac")
        chunks = [slice(c * GT, (c + 1) * GT) for c in range(NI // GT)]
        for c in range(len(chunks) + 2):
            if c < len(chunks):
                r = chunks[c]
                nc.vector.tensor_tensor(out=ang[:, r, :], in0=pos[:, r].unsqueeze(2).to_broadcast([P, GT, HALF]),
                                        in1=turns[:].unsqueeze(1).to_broadcast([P, GT, HALF]), op=ALU.mult)
            if 0 <= c - 1 < len(chunks):
                r = chunks[c - 1]
                nc.vector.tensor_scalar(out=whole[:, r, :], in0=ang[:, r, :], scalar1=MAGIC, scalar2=MAGIC, op0=ALU.add, op1=ALU.subtract)
            if 0 <= c - 2:
                r = chunks[c - 2]
                nc.vector.tensor_tensor(out=frac[:, r, :], in0=ang[:, r, :], in1=whole[:, r, :], op=ALU.subtract)
        sin_t = const.tile([P, NI, HALF], F32, name="sin_t")
        absf = const.tile([P, NI, HALF], F32, name="absf")
        tab = const.tile([P, NI, 3, HALF], F32, name="tab")

        wc = const.tile([P, 384], U32, name="wc", align_bytes=64)
        ws = const.tile([P, 384], U8, name="ws", align_bytes=64)
        wg_ab = const.tile([P, 1024], BF16, name="wg_ab", align_bytes=64)
        wg_c = const.tile([P, 512], BF16, name="wg_c", align_bytes=64)
        cast(0, FIRST)
        turn_first()
        turn(WORD[1])
        tw = ps_r.tile([P, 512], F32, name="tw", tag="mm")
        for a2, w_t in enumerate((w_a, w_b)):
            for u in range(2):
                nc.tensor.transpose(tw[:, u * 256 + a2 * P:u * 256 + (a2 + 1) * P], w_t[:].bitcast(F32)[:, u:256:2], ident[:])
        tw2 = ps_r.tile([P, 512], F32, name="tw2", tag="mm")
        for u in range(2):
            nc.tensor.transpose(tw2[:, u * P:(u + 1) * P], w_c[:].bitcast(F32)[:, u:256:2], ident[:])
        cast(1, (0, 2 * D, XW))
        table(0)
        cast(2, WHOLE)
        for c in range(1, NI // GT):
            table(c)

        for m in range(-6, NM):
            if m >= 0 and m % 2 == 0:
                finish_v(m // 2)
            if m >= 0:
                rope(m, 0)
                rope(m, 1)
                if m + 2 < NM:
                    add_up(m, nc.gpsimd)
                elif m + 1 == NM:
                    add_up(m - 1, nc.vector)
                    add_up(m, nc.vector)
            if m == -2:
                nc.vector.quantize_mx(out=wc[:, 0:256].bitcast(FP8X4), scales=ws[:, 0:256], in_=wg_ab[:])
                nc.vector.quantize_mx(out=wc[:, 256:384].bitcast(FP8X4), scales=ws[:, 256:384], in_=wg_c[:])
            if m % 2 == 0 and 0 <= m + 2 < NM:
                quant((m + 2) // 2)
            if 0 <= m + 2 < NM:
                mult(m + 2)
                if m % 2 == 1:
                    mult_v((m + 2) // 2)
            if m + 6 in PLANE:
                weave(m + 6)
            if m % 2 == 0 and 3 <= m // 2 + 5 < NG:
                cast(m // 2 + 5, WHOLE)
            if m + 8 in PLANE:
                turn_y(m + 8)
            if m == -4:
                scale_first()
                turn(WORD[2])
            elif m + 4 in WORD:
                scale_out(m + 4, P if m + 3 in PLANE else 0, 2 * P)
                k = WORD.index(m + 4) + 2
                if k < len(WORD):
                    turn(WORD[k])
            elif m + 4 in PLANE and m + 5 < NM:
                scale_out(m + 5, 0, P)
            if m == -3:
                nc.vector.tensor_copy(out=wg_ab[:].bitcast(F32).rearrange("p (r u) -> p r u", u=2),
                                      in_=tw[:].rearrange("p (u r) -> p r u", u=2))
                nc.vector.tensor_copy(out=wg_c[:].bitcast(F32).rearrange("p (r u) -> p r u", u=2),
                                      in_=tw2[:, 0:256].rearrange("p (u r) -> p r u", u=2))
